import numpy as np
import ml_dtypes


def mxq(x, axis, fmt="e4m3"):
    dtype, down = {"e4m3": (ml_dtypes.float8_e4m3fn, 7), "e5m2": (ml_dtypes.float8_e5m2, 14)}[fmt]
    v = np.moveaxis(np.asarray(x, np.float32).astype(ml_dtypes.bfloat16).astype(np.float64), axis, -1)
    blocks = v.reshape(v.shape[:-1] + (-1, 32))
    amax = np.abs(blocks).max(-1, keepdims=True)
    byte = np.maximum(np.where(amax > 0, np.frexp(amax)[1] - 1 + 127, 0) - down, 1)
    scale = np.exp2(byte - 127.0)
    codes = (blocks / scale).astype(np.float32).astype(dtype).astype(np.float64)
    return np.moveaxis((codes * scale).reshape(v.shape), -1, axis)


WIDE = False


def mx_kscale(k):
    if not WIDE:
        return np.ones(k)
    levels = np.array([10, -10, 5, -5, 0])
    if k % 512:
        return np.exp2(np.random.permutation(np.resize(levels, k // 32))).repeat(32)
    a = np.empty((k // 512, 16))
    for p in range(k // 512):
        a[p, :8] = np.random.permutation(np.resize(levels, 8))
        for g in range(8):
            far = levels[np.abs(levels - a[p, g]) >= 10]
            a[p, g + 8] = far[np.random.randint(len(far))]
    return np.exp2(a.ravel()).repeat(32)


BF16 = ml_dtypes.bfloat16


def bf(x):
    return np.asarray(x, np.float32).astype(BF16)


def f64(x):
    return np.asarray(x).astype(np.float64)


B, S, D, DI = 4, 512, 512, 2048
EPS = 1e-12


def l2norm(v):
    n = np.sqrt(np.sum(v * v, axis=-1, keepdims=True))
    return v / np.maximum(n, EPS)


def setup_inputs():
    s = mx_kscale(D)
    return {"x": bf(np.random.standard_normal((B, S, D)) * s),
            "wk": bf(np.random.standard_normal((D, DI)) / np.sqrt(D) / s[:, None]),
            "wv": bf(np.random.standard_normal((D, DI)) / np.sqrt(D) / s[:, None])}


def reference(x, wk, wv):
    xq = mxq(f64(x), 2, "e4m3")
    k = l2norm(xq @ mxq(f64(wk), 0, "e4m3"))
    v = xq @ mxq(f64(wv), 0, "e4m3")
    return np.sum(k * v, axis=-2, keepdims=True)

@@ -1,0 +1,278 @@
+from contextlib import ExitStack
+
+import concourse.mybir as mybir
+from concourse.masks import make_identity
+
+F32 = mybir.dt.float32
+BF16 = mybir.dt.bfloat16
+U32 = mybir.dt.uint32
+U8 = mybir.dt.uint8
+FP8X4 = mybir.dt.float8_e4m3fn_x4
+ALU = mybir.AluOpType
+ACT = mybir.ActivationFunctionType
+AXIS = mybir.AxisListType
+
+P = 128
+PACK = 4
+BATCHES = 4
+TOKENS = 512
+FEATURES = 512
+WIDTH = 2048
+EPS = 1e-12
+CHUNK = 512
+CHUNKS = WIDTH // CHUNK
+BLOCKS = CHUNK // P
+TILES_PER_BATCH = TOKENS // P
+TILES = BATCHES * TILES_PER_BATCH
+VALUE_LAG = 2
+SUM_LAG = TILES_PER_BATCH
+
+FLOPS = 2 * 2 * BATCHES * TOKENS * FEATURES * WIDTH
+
+
+def tile_hydraencoderlayer_pa_kernel(tc, x, wk, wv, out):
+    nc = tc.nc
+    with ExitStack() as ctx:
+        ctx.enter_context(tc.manual_schedule())
+        keep = ctx.enter_context(tc.tile_pool(name="keep", bufs=1))
+        raw_pool = ctx.enter_context(tc.tile_pool(name="raw", bufs=2 * CHUNKS))
+        grouped_pool = ctx.enter_context(tc.tile_pool(name="grouped", bufs=4))
+        key_pool = ctx.enter_context(tc.tile_pool(name="keys", bufs=VALUE_LAG + 2))
+        square_pool = ctx.enter_context(tc.tile_pool(name="squares", bufs=2))
+        norm_pool = ctx.enter_context(tc.tile_pool(name="norms", bufs=VALUE_LAG + 2))
+        product_pool = ctx.enter_context(tc.tile_pool(name="products", bufs=2 * CHUNKS))
+        batch_pool = ctx.enter_context(tc.tile_pool(name="batch_sums", bufs=2))
+        key_banks = ctx.enter_context(tc.psum_pool(name="key_banks", bufs=4))
+        value_banks = ctx.enter_context(tc.psum_pool(name="value_banks", bufs=4))
+
+        x_raw = keep.tile([P, BATCHES, TILES_PER_BATCH, FEATURES], BF16)
+
+        def load_x(b):
+            nc.sync.dma_start(
+                out=x_raw[:, b], in_=x[b].rearrange("(p t) k -> p t k", t=TILES_PER_BATCH)
+            )
+
+        def load_weight_chunk(w, c):
+            raw = raw_pool.tile([P, PACK, CHUNK], BF16, tag="raw")
+            nc.sync.dma_start(
+                out=raw[:],
+                in_=w[:, c * CHUNK : (c + 1) * CHUNK].rearrange("(p t) c -> p t c", t=PACK),
+            )
+            return raw
+
+        load_x(0)
+        wk_raw = [load_weight_chunk(wk, c) for c in range(CHUNKS)]
+        load_x(1)
+        wv_raw = [load_weight_chunk(wv, c) for c in range(CHUNKS)]
+        load_x(2)
+        load_x(3)
+
+        identity = keep.tile([P, P], F32)
+        make_identity(nc, identity[:])
+        sums = keep.tile([P, P], F32)
+        nc.vector.memset(sums[:], 0.0)
+        one = keep.tile([P, 1], F32)
+        nc.vector.memset(one[:], 1.0)
+        nc.scalar.sqrt(out=one[:], in_=one[:])
+
+        x_codes = keep.tile([P, TILES * P], U32, align_bytes=64)
+        x_scales = keep.tile([P, TILES * P], U8, align_bytes=64)
+        wk_codes = keep.tile([P, WIDTH], U32, align_bytes=64)
+        wk_scales = keep.tile([P, WIDTH], U8, align_bytes=64)
+        wv_codes = keep.tile([P, WIDTH], U32, align_bytes=64)
+        wv_scales = keep.tile([P, WIDTH], U8, align_bytes=64)
+
+        def quantise_x(b):
+            x_words = x_raw[:].bitcast(F32)
+            x_grouped = grouped_pool.tile(
+                [P, TOKENS, PACK], BF16, tag="x_grouped", bufs=2, align_bytes=64
+            )
+            grouped_words = x_grouped[:].bitcast(F32)
+            for half in range(2):
+                flipped = key_banks.tile([P, 2, 2, P], F32, tag="bank")
+                for i in range(2):
+                    for u in range(2):
+                        nc.tensor.transpose(
+                            flipped[:, i, u, :],
+                            x_words[:, b, 2 * half + i, u : FEATURES // 2 : 2],
+                            identity[:],
+                        )
+                nc.vector.tensor_copy(
+                    out=grouped_words[:, 2 * half * P : 2 * (half + 1) * P, :].rearrange(
+                        "p (i k) u -> p i k u", i=2
+                    ),
+                    in_=flipped[:].rearrange("p i u k -> p i k u"),
+                )
+            columns = slice(b * TOKENS, (b + 1) * TOKENS)
+            nc.vector.quantize_mx(
+                out=x_codes[:, columns].bitcast(FP8X4),
+                scales=x_scales[:, columns],
+                in_=x_grouped[:].rearrange("p k t -> p (k t)"),
+            )
+
+        def regroup_weight_chunk(raw, copy):
+            grouped = grouped_pool.tile([P, CHUNK, PACK], BF16, tag="w_grouped", align_bytes=64)
+            copy(
+                out=grouped[:].rearrange("p (c i) t -> p c t i", i=4),
+                in_=raw[:].rearrange("p t (c i) -> p c t i", i=4),
+            )
+            return grouped
+
+        def quantise_weight_chunk(grouped, codes, scales, c):
+            columns = slice(c * CHUNK, (c + 1) * CHUNK)
+            nc.vector.quantize_mx(
+                out=codes[:, columns].bitcast(FP8X4),
+                scales=scales[:, columns],
+                in_=grouped[:].rearrange("p c t -> p (c t)"),
+            )
+
+        def quantise_weight(raws, codes, scales, first, count, odd_copy):
+            grouped = [None] * CHUNKS
+            for c in range(first, first + count + 1):
+                if c < first + count:
+                    copy = odd_copy if c % 2 == 1 else nc.vector.tensor_copy
+                    grouped[c] = regroup_weight_chunk(raws[c], copy)
+                if c > first:
+                    quantise_weight_chunk(grouped[c - 1], codes, scales, c - 1)
+
+        keys = [None] * TILES
+        norms_squared = [None] * TILES
+        norms = [None] * TILES
+        inverse_norms = [None] * TILES
+        first_three = [None] * BATCHES
+        fourth = [None] * BATCHES
+
+        def key_products(t):
+            tokens = slice(t * P, (t + 1) * P)
+            keys[t] = key_pool.tile([P, WIDTH], F32, name="a_sb", tag="a_sb")
+            for c in range(CHUNKS):
+                columns = slice(c * CHUNK, (c + 1) * CHUNK)
+                a_bank = key_banks.tile([P, CHUNK], F32, tag="bank")
+                nc.tensor.matmul_mx(
+                    out=a_bank[:],
+                    lhsT=x_codes[:, tokens].bitcast(FP8X4),
+                    lhsT_scale=x_scales[:, tokens],
+                    rhs=wk_codes[:, columns].bitcast(FP8X4),
+                    rhs_scale=wk_scales[:, columns],
+                    start=True,
+                    stop=True,
+                )
+                if c == 0:
+                    nc.vector.tensor_copy(out=keys[t][:, columns], in_=a_bank[:])
+                else:
+                    nc.scalar.copy(out=keys[t][:, columns], in_=a_bank[:])
+
+        def sum_of_squares(t):
+            squares = square_pool.tile([P, WIDTH], BF16, tag="squares")
+            norms_squared[t] = norm_pool.tile([P, 1], F32, name="norm_squared", tag="norm_squared")
+            nc.scalar.activation(
+                out=squares[:], in_=keys[t][:], func=ACT.Square, accum_out=norms_squared[t][:]
+            )
+
+        def clamp_and_root(t):
+            clamped = norm_pool.tile([P, 1], F32, tag="clamped")
+            nc.vector.tensor_scalar_max(out=clamped[:], in0=norms_squared[t][:], scalar1=EPS * EPS)
+            norms[t] = norm_pool.tile([P, 1], F32, name="norm", tag="norm")
+            nc.scalar.sqrt(out=norms[t][:], in_=clamped[:])
+
+        def invert_norm(t):
+            inverse_norms[t] = norm_pool.tile([P, 1], F32, name="inverse_norm", tag="inverse_norm")
+            nc.vector.reciprocal(out=inverse_norms[t][:], in_=norms[t][:])
+
+        def value_stage(t):
+            b, place = divmod(t, TILES_PER_BATCH)
+            tokens = slice(t * P, (t + 1) * P)
+            if place == 0:
+                first_three[b] = batch_pool.tile([P, WIDTH], F32, name="first_three", tag="first_three")
+            if place == TILES_PER_BATCH - 1:
+                fourth[b] = batch_pool.tile([P, WIDTH], F32, name="fourth", tag="fourth")
+            for c in range(CHUNKS):
+                columns = slice(c * CHUNK, (c + 1) * CHUNK)
+                v_bank = value_banks.tile([P, CHUNK], F32, tag="bank")
+                nc.tensor.matmul_mx(
+                    out=v_bank[:],
+                    lhsT=x_codes[:, tokens].bitcast(FP8X4),
+                    lhsT_scale=x_scales[:, tokens],
+                    rhs=wv_codes[:, columns].bitcast(FP8X4),
+                    rhs_scale=wv_scales[:, columns],
+                    start=True,
+                    stop=True,
+                )
+                if place == 0:
+                    product = first_three[b][:, columns]
+                elif place == TILES_PER_BATCH - 1:
+                    product = fourth[b][:, columns]
+                else:
+                    product_tile = product_pool.tile([P, CHUNK], F32, tag="product")
+                    product = product_tile[:]
+                nc.vector.scalar_tensor_tensor(
+                    out=product,
+                    in0=v_bank[:],
+                    scalar=inverse_norms[t][:],
+                    in1=keys[t][:, columns],
+                    op0=ALU.mult,
+                    op1=ALU.mult,
+                )
+                if 0 < place < TILES_PER_BATCH - 1:
+                    nc.gpsimd.tensor_tensor(
+                        out=first_three[b][:, columns],
+                        in0=first_three[b][:, columns],
+                        in1=product,
+                        op=ALU.add,
+                    )
+
+        def sum_over_tokens(m):
+            b, c = divmod(m, CHUNKS)
+            turned = value_banks.tile([P, BLOCKS, P], F32, tag="bank")
+            for j in range(BLOCKS):
+                block = slice(c * CHUNK + j * P, c * CHUNK + (j + 1) * P)
+                nc.tensor.matmul(
+                    out=turned[:, j, :],
+                    lhsT=first_three[b][:, block],
+                    rhs=identity[:],
+                    is_transpose=True,
+                    start=True,
+                    stop=False,
+                )
+                nc.tensor.matmul(
+                    out=turned[:, j, :],
+                    lhsT=fourth[b][:, block],
+                    rhs=identity[:],
+                    is_transpose=True,
+                    start=False,
+                    stop=True,
+                )
+            nc.vector.tensor_reduce(
+                out=sums[:, m * BLOCKS : (m + 1) * BLOCKS], in_=turned[:], axis=AXIS.X, op=ALU.add
+            )
+
+        def is_tile(t):
+            return 0 <= t < TILES
+
+        quantise_x(0)
+        quantise_weight(wk_raw, wk_codes, wk_scales, 0, CHUNKS, nc.scalar.copy)
+        for t in range(TILES + VALUE_LAG + SUM_LAG):
+            if is_tile(t):
+                key_products(t)
+            if is_tile(t - 1):
+                clamp_and_root(t - 1)
+            if is_tile(t):
+                sum_of_squares(t)
+            if t < VALUE_LAG:
+                share = CHUNKS // VALUE_LAG
+                quantise_weight(wv_raw, wv_codes, wv_scales, t * share, share, nc.vector.tensor_copy)
+            if is_tile(t - VALUE_LAG):
+                value_stage(t - VALUE_LAG)
+            if is_tile(t - 1):
+                invert_norm(t - 1)
+            if is_tile(t) and t % TILES_PER_BATCH == 2 and t // TILES_PER_BATCH + 1 < BATCHES:
+                quantise_x(t // TILES_PER_BATCH + 1)
+            if is_tile(t - VALUE_LAG - SUM_LAG):
+                sum_over_tokens(t - VALUE_LAG - SUM_LAG)
+
+        rows = BATCHES * CHUNKS * BLOCKS
+        turned_sums = key_banks.tile([P, P], F32, tag="bank")
+        nc.tensor.transpose(turned_sums[:], sums[:], identity[:])
+        result = keep.tile([P, P], F32)
+        nc.vector.tensor_copy(out=result[:], in_=turned_sums[:])
+        nc.sync.dma_start(out=out.rearrange("b o (r p) -> (b o r) p", p=P), in_=result[0:rows, :])

@@ -22,10 +22,15 @@ EPS = 1e-12
 CHUNK = 512
 CHUNKS = WIDTH // CHUNK
 BLOCKS = CHUNK // P
-TILES_PER_BATCH = TOKENS // P
-TILES = BATCHES * TILES_PER_BATCH
-VALUE_LAG = 2
-SUM_LAG = TILES_PER_BATCH
+TILES = BATCHES * TOKENS // P
+VALUE_LAG = 3
+
+GROUPS = (
+    ((0, 1), (2, 3), (4, 5), (6, 7)),
+    ((8, 9, 10, 11, 12, 13), (14,), (15,)),
+)
+LAST_ADDED = 14
+FIRST_GROUP_SUM = 11
 
 FLOPS = 2 * 2 * BATCHES * TOKENS * FEATURES * WIDTH
 
@@ -40,17 +45,17 @@ def tile_hydraencoderlayer_pa_kernel(tc, x, wk, wv, out):
         key_pool = ctx.enter_context(tc.tile_pool(name="keys", bufs=VALUE_LAG + 2))
         square_pool = ctx.enter_context(tc.tile_pool(name="squares", bufs=2))
         norm_pool = ctx.enter_context(tc.tile_pool(name="norms", bufs=VALUE_LAG + 2))
-        product_pool = ctx.enter_context(tc.tile_pool(name="products", bufs=2 * CHUNKS))
-        batch_pool = ctx.enter_context(tc.tile_pool(name="batch_sums", bufs=2))
-        key_banks = ctx.enter_context(tc.psum_pool(name="key_banks", bufs=4))
-        value_banks = ctx.enter_context(tc.psum_pool(name="value_banks", bufs=4))
+        product_pool = ctx.enter_context(tc.tile_pool(name="products", bufs=2))
+        addend_pool = ctx.enter_context(tc.tile_pool(name="addends", bufs=6))
+        scalar_banks = ctx.enter_context(tc.psum_pool(name="scalar_banks", bufs=4))
+        vector_banks = ctx.enter_context(tc.psum_pool(name="vector_banks", bufs=4))
 
-        x_raw = keep.tile([P, BATCHES, TILES_PER_BATCH, FEATURES], BF16)
+        x_raw = keep.tile([P, TILES, FEATURES], BF16)
+        x_rows = x.flatten_outer_dims().rearrange("(p t) k -> p t k", t=TILES)
 
-        def load_x(b):
-            nc.sync.dma_start(
-                out=x_raw[:, b], in_=x[b].rearrange("(p t) k -> p t k", t=TILES_PER_BATCH)
-            )
+        def load_x(first, count):
+            tiles = slice(first, first + count)
+            nc.sync.dma_start(out=x_raw[:, tiles, :], in_=x_rows[:, tiles, :])
 
         def load_weight_chunk(w, c):
             raw = raw_pool.tile([P, PACK, CHUNK], BF16, tag="raw")
@@ -60,21 +65,22 @@ def tile_hydraencoderlayer_pa_kernel(tc, x, wk, wv, out):
             )
             return raw
 
-        load_x(0)
+        load_x(0, 1)
         wk_raw = [load_weight_chunk(wk, c) for c in range(CHUNKS)]
-        load_x(1)
+        load_x(1, 3)
         wv_raw = [load_weight_chunk(wv, c) for c in range(CHUNKS)]
-        load_x(2)
-        load_x(3)
+        for first in range(4, TILES, 4):
+            load_x(first, 4)
 
         identity = keep.tile([P, P], F32)
         make_identity(nc, identity[:])
-        sums = keep.tile([P, P], F32)
-        nc.vector.memset(sums[:], 0.0)
+        sums = []
+        for g in range(len(GROUPS)):
+            sums.append(keep.tile([P, P], F32, name="sums" + str(g)))
+            nc.gpsimd.memset(sums[g][:], 0.0)
         one = keep.tile([P, 1], F32)
         nc.vector.memset(one[:], 1.0)
-        nc.scalar.sqrt(out=one[:], in_=one[:])
-
+        nc.scalar.activation(out=one[:], in_=one[:], func=ACT.Abs_reciprocal_sqrt)
         x_codes = keep.tile([P, TILES * P], U32, align_bytes=64)
         x_scales = keep.tile([P, TILES * P], U8, align_bytes=64)
         wk_codes = keep.tile([P, WIDTH], U32, align_bytes=64)
@@ -82,32 +88,30 @@ def tile_hydraencoderlayer_pa_kernel(tc, x, wk, wv, out):
         wv_codes = keep.tile([P, WIDTH], U32, align_bytes=64)
         wv_scales = keep.tile([P, WIDTH], U8, align_bytes=64)
 
-        def quantise_x(b):
+        def regroup_x(first, count, copy):
+            grouped = grouped_pool.tile([P, 2 * P, PACK], BF16, tag="x_grouped", bufs=3, align_bytes=64)
             x_words = x_raw[:].bitcast(F32)
-            x_grouped = grouped_pool.tile(
-                [P, TOKENS, PACK], BF16, tag="x_grouped", bufs=2, align_bytes=64
+            grouped_words = grouped[:].bitcast(F32)
+            flipped = vector_banks.tile([P, 2, 2, P], F32, tag="bank")
+            for n in range(count):
+                for u in range(2):
+                    nc.tensor.transpose(
+                        flipped[:, n, u, :],
+                        x_words[:, first + n, u : FEATURES // 2 : 2],
+                        identity[:],
+                    )
+            copy(
+                out=grouped_words[:, 0 : count * P, :].rearrange("p (n k) u -> p n k u", n=count),
+                in_=flipped[:, 0:count].rearrange("p n u k -> p n k u"),
             )
-            grouped_words = x_grouped[:].bitcast(F32)
-            for half in range(2):
-                flipped = key_banks.tile([P, 2, 2, P], F32, tag="bank")
-                for i in range(2):
-                    for u in range(2):
-                        nc.tensor.transpose(
-                            flipped[:, i, u, :],
-                            x_words[:, b, 2 * half + i, u : FEATURES // 2 : 2],
-                            identity[:],
-                        )
-                nc.vector.tensor_copy(
-                    out=grouped_words[:, 2 * half * P : 2 * (half + 1) * P, :].rearrange(
-                        "p (i k) u -> p i k u", i=2
-                    ),
-                    in_=flipped[:].rearrange("p i u k -> p i k u"),
-                )
-            columns = slice(b * TOKENS, (b + 1) * TOKENS)
+            return grouped
+
+        def quantise_x(grouped, first, count):
+            columns = slice(first * P, (first + count) * P)
             nc.vector.quantize_mx(
                 out=x_codes[:, columns].bitcast(FP8X4),
                 scales=x_scales[:, columns],
-                in_=x_grouped[:].rearrange("p k t -> p (k t)"),
+                in_=grouped[:, 0 : count * P, :].rearrange("p k t -> p (k t)"),
             )
 
         def regroup_weight_chunk(raw, copy):
@@ -126,41 +130,36 @@ def tile_hydraencoderlayer_pa_kernel(tc, x, wk, wv, out):
                 in_=grouped[:].rearrange("p c t -> p (c t)"),
             )
 
-        def quantise_weight(raws, codes, scales, first, count, odd_copy):
-            grouped = [None] * CHUNKS
-            for c in range(first, first + count + 1):
-                if c < first + count:
-                    copy = odd_copy if c % 2 == 1 else nc.vector.tensor_copy
-                    grouped[c] = regroup_weight_chunk(raws[c], copy)
-                if c > first:
-                    quantise_weight_chunk(grouped[c - 1], codes, scales, c - 1)
-
         keys = [None] * TILES
         norms_squared = [None] * TILES
-        norms = [None] * TILES
+        roots = [None] * TILES
         inverse_norms = [None] * TILES
-        first_three = [None] * BATCHES
-        fourth = [None] * BATCHES
+        v_copy = nc.vector.tensor_copy
+        s_copy = nc.scalar.copy
+        products = [None] * TILES
+        addend_of = {}
+        for g in range(len(GROUPS)):
+            for members in GROUPS[g]:
+                for t in members:
+                    addend_of[t] = members
 
-        def key_products(t):
+        def key_chunk(t, c, on_vector):
             tokens = slice(t * P, (t + 1) * P)
-            keys[t] = key_pool.tile([P, WIDTH], F32, name="a_sb", tag="a_sb")
-            for c in range(CHUNKS):
-                columns = slice(c * CHUNK, (c + 1) * CHUNK)
-                a_bank = key_banks.tile([P, CHUNK], F32, tag="bank")
-                nc.tensor.matmul_mx(
-                    out=a_bank[:],
-                    lhsT=x_codes[:, tokens].bitcast(FP8X4),
-                    lhsT_scale=x_scales[:, tokens],
-                    rhs=wk_codes[:, columns].bitcast(FP8X4),
-                    rhs_scale=wk_scales[:, columns],
-                    start=True,
-                    stop=True,
-                )
-                if c == 0:
-                    nc.vector.tensor_copy(out=keys[t][:, columns], in_=a_bank[:])
-                else:
-                    nc.scalar.copy(out=keys[t][:, columns], in_=a_bank[:])
+            columns = slice(c * CHUNK, (c + 1) * CHUNK)
+            if keys[t] is None:
+                keys[t] = key_pool.tile([P, WIDTH], F32, name="a_sb", tag="a_sb")
+            banks, copy = (vector_banks, v_copy) if on_vector else (scalar_banks, s_copy)
+            a_bank = banks.tile([P, CHUNK], F32, name="a_bank", tag="bank")
+            nc.tensor.matmul_mx(
+                out=a_bank[:],
+                lhsT=x_codes[:, tokens].bitcast(FP8X4),
+                lhsT_scale=x_scales[:, tokens],
+                rhs=wk_codes[:, columns].bitcast(FP8X4),
+                rhs_scale=wk_scales[:, columns],
+                start=True,
+                stop=True,
+            )
+            copy(out=keys[t][:, columns], in_=a_bank[:])
 
         def sum_of_squares(t):
             squares = square_pool.tile([P, WIDTH], BF16, tag="squares")
@@ -169,110 +168,162 @@ def tile_hydraencoderlayer_pa_kernel(tc, x, wk, wv, out):
                 out=squares[:], in_=keys[t][:], func=ACT.Square, accum_out=norms_squared[t][:]
             )
 
-        def clamp_and_root(t):
-            clamped = norm_pool.tile([P, 1], F32, tag="clamped")
-            nc.vector.tensor_scalar_max(out=clamped[:], in0=norms_squared[t][:], scalar1=EPS * EPS)
-            norms[t] = norm_pool.tile([P, 1], F32, name="norm", tag="norm")
-            nc.scalar.sqrt(out=norms[t][:], in_=clamped[:])
+        def root_norm(t):
+            roots[t] = norm_pool.tile([P, 1], F32, name="root", tag="root")
+            nc.scalar.activation(out=roots[t][:], in_=norms_squared[t][:], func=ACT.Abs_reciprocal_sqrt)
 
-        def invert_norm(t):
+        def limit_norm(t):
             inverse_norms[t] = norm_pool.tile([P, 1], F32, name="inverse_norm", tag="inverse_norm")
-            nc.vector.reciprocal(out=inverse_norms[t][:], in_=norms[t][:])
+            nc.vector.tensor_scalar_min(out=inverse_norms[t][:], in0=roots[t][:], scalar1=1.0 / EPS)
 
-        def value_stage(t):
-            b, place = divmod(t, TILES_PER_BATCH)
+        def value_chunk(t, c):
             tokens = slice(t * P, (t + 1) * P)
-            if place == 0:
-                first_three[b] = batch_pool.tile([P, WIDTH], F32, name="first_three", tag="first_three")
-            if place == TILES_PER_BATCH - 1:
-                fourth[b] = batch_pool.tile([P, WIDTH], F32, name="fourth", tag="fourth")
-            for c in range(CHUNKS):
-                columns = slice(c * CHUNK, (c + 1) * CHUNK)
-                v_bank = value_banks.tile([P, CHUNK], F32, tag="bank")
-                nc.tensor.matmul_mx(
-                    out=v_bank[:],
-                    lhsT=x_codes[:, tokens].bitcast(FP8X4),
-                    lhsT_scale=x_scales[:, tokens],
-                    rhs=wv_codes[:, columns].bitcast(FP8X4),
-                    rhs_scale=wv_scales[:, columns],
-                    start=True,
-                    stop=True,
-                )
-                if place == 0:
-                    product = first_three[b][:, columns]
-                elif place == TILES_PER_BATCH - 1:
-                    product = fourth[b][:, columns]
+            columns = slice(c * CHUNK, (c + 1) * CHUNK)
+            members = addend_of[t]
+            if c == 0:
+                if t == members[0]:
+                    products[t] = addend_pool.tile([P, WIDTH], F32, name="addend", tag="addend")
                 else:
-                    product_tile = product_pool.tile([P, CHUNK], F32, tag="product")
-                    product = product_tile[:]
-                nc.vector.scalar_tensor_tensor(
-                    out=product,
-                    in0=v_bank[:],
-                    scalar=inverse_norms[t][:],
-                    in1=keys[t][:, columns],
-                    op0=ALU.mult,
-                    op1=ALU.mult,
-                )
-                if 0 < place < TILES_PER_BATCH - 1:
-                    nc.gpsimd.tensor_tensor(
-                        out=first_three[b][:, columns],
-                        in0=first_three[b][:, columns],
-                        in1=product,
-                        op=ALU.add,
-                    )
+                    products[t] = product_pool.tile([P, WIDTH], F32, name="product", tag="product")
+            v_bank = vector_banks.tile([P, CHUNK], F32, tag="bank")
+            nc.tensor.matmul_mx(
+                out=v_bank[:],
+                lhsT=x_codes[:, tokens].bitcast(FP8X4),
+                lhsT_scale=x_scales[:, tokens],
+                rhs=wv_codes[:, columns].bitcast(FP8X4),
+                rhs_scale=wv_scales[:, columns],
+                start=True,
+                stop=True,
+            )
+            nc.vector.scalar_tensor_tensor(
+                out=products[t][:, columns],
+                in0=v_bank[:],
+                scalar=inverse_norms[t][:],
+                in1=keys[t][:, columns],
+                op0=ALU.mult,
+                op1=ALU.mult,
+            )
 
-        def sum_over_tokens(m):
-            b, c = divmod(m, CHUNKS)
-            turned = value_banks.tile([P, BLOCKS, P], F32, tag="bank")
+        def add_product(t, c):
+            step = 1 if t >= LAST_ADDED else 2
+            members = addend_of[t]
+            if t != members[0] and c % step == step - 1:
+                columns = slice((c + 1 - step) * CHUNK, (c + 1) * CHUNK)
+                addend = products[members[0]][:, columns]
+                nc.gpsimd.tensor_tensor(
+                    out=addend, in0=addend, in1=products[t][:, columns], op=ALU.add
+                )
+
+        def turn_and_add(g, c, banks):
+            turned = banks.tile([P, BLOCKS, P], F32, name="turned", tag="bank")
+            addends = GROUPS[g]
             for j in range(BLOCKS):
                 block = slice(c * CHUNK + j * P, c * CHUNK + (j + 1) * P)
-                nc.tensor.matmul(
-                    out=turned[:, j, :],
-                    lhsT=first_three[b][:, block],
-                    rhs=identity[:],
-                    is_transpose=True,
-                    start=True,
-                    stop=False,
-                )
-                nc.tensor.matmul(
-                    out=turned[:, j, :],
-                    lhsT=fourth[b][:, block],
-                    rhs=identity[:],
-                    is_transpose=True,
-                    start=False,
-                    stop=True,
-                )
+                for n in range(len(addends)):
+                    nc.tensor.matmul(
+                        out=turned[:, j, :],
+                        lhsT=products[addends[n][0]][:, block],
+                        rhs=identity[:],
+                        is_transpose=True,
+                        start=n == 0,
+                        stop=n == len(addends) - 1,
+                    )
+            return turned
+
+        def sum_over_tokens(g, c, turned):
+            by_batch = sums[g][:, 0 : BATCHES * CHUNKS * BLOCKS].rearrange("p (b r) -> p r b", b=BATCHES)
             nc.vector.tensor_reduce(
-                out=sums[:, m * BLOCKS : (m + 1) * BLOCKS], in_=turned[:], axis=AXIS.X, op=ALU.add
+                out=by_batch[:, c * BLOCKS : (c + 1) * BLOCKS, :],
+                in_=turned[:].rearrange("p j (b q) -> p j b q", b=BATCHES),
+                axis=AXIS.X,
+                op=ALU.add,
             )
 
         def is_tile(t):
             return 0 <= t < TILES
 
-        quantise_x(0)
-        quantise_weight(wk_raw, wk_codes, wk_scales, 0, CHUNKS, nc.scalar.copy)
-        for t in range(TILES + VALUE_LAG + SUM_LAG):
+        def vector_key_chunks(t):
+            return range(0) if t < 4 else range(1)
+
+        def values_done(t):
+            return max(0, min(t, TILES, 2 * t - 5))
+
+        wk_grouped = [None] * CHUNKS
+        wv_grouped = [None] * CHUNKS
+        x_first = regroup_x(0, 1, v_copy)
+        wk_grouped[1] = regroup_weight_chunk(wk_raw[1], s_copy)
+        wk_grouped[0] = regroup_weight_chunk(wk_raw[0], v_copy)
+        quantise_x(x_first, 0, 1)
+        quantise_weight_chunk(wk_grouped[0], wk_codes, wk_scales, 0)
+        key_chunk(0, 0, False)
+        wk_grouped[2] = regroup_weight_chunk(wk_raw[2], v_copy)
+        quantise_weight_chunk(wk_grouped[1], wk_codes, wk_scales, 1)
+        key_chunk(0, 1, False)
+        wk_grouped[3] = regroup_weight_chunk(wk_raw[3], v_copy)
+        for c in range(2, CHUNKS):
+            quantise_weight_chunk(wk_grouped[c], wk_codes, wk_scales, c)
+            key_chunk(0, c, False)
+        sum_of_squares(0)
+        x_second = regroup_x(1, 1, v_copy)
+        grouped_x = regroup_x(2, 2, v_copy)
+        quantise_x(x_second, 1, 1)
+        quantise_x(grouped_x, 2, 2)
+        wv_grouped[0] = regroup_weight_chunk(wv_raw[0], v_copy)
+        wv_grouped[1] = regroup_weight_chunk(wv_raw[1], v_copy)
+        grouped_x = regroup_x(4, 2, v_copy)
+        quantise_weight_chunk(wv_grouped[0], wv_codes, wv_scales, 0)
+        wv_grouped[2] = regroup_weight_chunk(wv_raw[2], v_copy)
+        quantise_weight_chunk(wv_grouped[1], wv_codes, wv_scales, 1)
+        wv_grouped[3] = regroup_weight_chunk(wv_raw[3], v_copy)
+        quantise_weight_chunk(wv_grouped[2], wv_codes, wv_scales, 2)
+        quantise_x(grouped_x, 4, 2)
+        quantise_weight_chunk(wv_grouped[3], wv_codes, wv_scales, 3)
+
+        for t in range(1, TILES + 1):
             if is_tile(t):
-                key_products(t)
-            if is_tile(t - 1):
-                clamp_and_root(t - 1)
-            if is_tile(t):
+                for c in range(CHUNKS):
+                    if c not in vector_key_chunks(t):
+                        key_chunk(t, c, False)
+                    if c == vector_key_chunks(t).stop:
+                        root_norm(t - 1)
                 sum_of_squares(t)
-            if t < VALUE_LAG:
-                share = CHUNKS // VALUE_LAG
-                quantise_weight(wv_raw, wv_codes, wv_scales, t * share, share, nc.vector.tensor_copy)
-            if is_tile(t - VALUE_LAG):
-                value_stage(t - VALUE_LAG)
-            if is_tile(t - 1):
-                invert_norm(t - 1)
-            if is_tile(t) and t % TILES_PER_BATCH == 2 and t // TILES_PER_BATCH + 1 < BATCHES:
-                quantise_x(t // TILES_PER_BATCH + 1)
-            if is_tile(t - VALUE_LAG - SUM_LAG):
-                sum_over_tokens(t - VALUE_LAG - SUM_LAG)
+            else:
+                root_norm(t - 1)
+            first_group_chunk = t - FIRST_GROUP_SUM
+            summing = 0 <= first_group_chunk < CHUNKS
+            if is_tile(t + 1):
+                for c in vector_key_chunks(t + 1):
+                    key_chunk(t + 1, c, True)
+            if summing:
+                turned = turn_and_add(0, first_group_chunk, vector_banks)
+            if t % 2 == 0 and is_tile(t + 4):
+                grouped_x = regroup_x(t + 4, 2, v_copy)
+            for v in range(values_done(t - 1), values_done(t)):
+                limit_norm(v)
+                for c in range(CHUNKS):
+                    value_chunk(v, c)
+                    add_product(v, c)
+                    if c > 0 and v == TILES - 1:
+                        turned = turn_and_add(1, c - 1, scalar_banks)
+                        sum_over_tokens(1, c - 1, turned)
+            if t % 2 == 1 and t > 1 and is_tile(t + 3):
+                quantise_x(grouped_x, t + 3, 2)
+            if summing:
+                sum_over_tokens(0, first_group_chunk, turned)
+        turned = turn_and_add(1, CHUNKS - 1, scalar_banks)
+        sum_over_tokens(1, CHUNKS - 1, turned)
 
         rows = BATCHES * CHUNKS * BLOCKS
-        turned_sums = key_banks.tile([P, P], F32, tag="bank")
-        nc.tensor.transpose(turned_sums[:], sums[:], identity[:])
+        turned_sums = scalar_banks.tile([P, P], F32, tag="bank")
+        for g in range(len(GROUPS)):
+            nc.tensor.matmul(
+                out=turned_sums[:],
+                lhsT=sums[g][:],
+                rhs=identity[:],
+                is_transpose=True,
+                start=g == 0,
+                stop=g == len(GROUPS) - 1,
+            )
         result = keep.tile([P, P], F32)
         nc.vector.tensor_copy(out=result[:], in_=turned_sums[:])
         nc.sync.dma_start(out=out.rearrange("b o (r p) -> (b o r) p", p=P), in_=result[0:rows, :])

@@ -81,6 +81,10 @@ def tile_hydraencoderlayer_pa_kernel(tc, x, wk, wv, out):
         one = keep.tile([P, 1], F32)
         nc.vector.memset(one[:], 1.0)
         nc.scalar.activation(out=one[:], in_=one[:], func=ACT.Abs_reciprocal_sqrt)
+        floor = keep.tile([P, 1], F32)
+        nc.vector.memset(floor[:], EPS * EPS)
+        minus_floor = keep.tile([P, 1], F32)
+        nc.vector.memset(minus_floor[:], -EPS * EPS)
         x_codes = keep.tile([P, TILES * P], U32, align_bytes=64)
         x_scales = keep.tile([P, TILES * P], U8, align_bytes=64)
         wk_codes = keep.tile([P, WIDTH], U32, align_bytes=64)
@@ -132,7 +136,7 @@ def tile_hydraencoderlayer_pa_kernel(tc, x, wk, wv, out):
 
         keys = [None] * TILES
         norms_squared = [None] * TILES
-        roots = [None] * TILES
+        excess = [None] * TILES
         inverse_norms = [None] * TILES
         v_copy = nc.vector.tensor_copy
         s_copy = nc.scalar.copy
@@ -168,13 +172,17 @@ def tile_hydraencoderlayer_pa_kernel(tc, x, wk, wv, out):
                 out=squares[:], in_=keys[t][:], func=ACT.Square, accum_out=norms_squared[t][:]
             )
 
-        def root_norm(t):
-            roots[t] = norm_pool.tile([P, 1], F32, name="root", tag="root")
-            nc.scalar.activation(out=roots[t][:], in_=norms_squared[t][:], func=ACT.Abs_reciprocal_sqrt)
-
         def limit_norm(t):
+            excess[t] = norm_pool.tile([P, 1], F32, name="excess", tag="excess")
+            nc.scalar.activation(
+                out=excess[t][:], in_=norms_squared[t][:], func=ACT.Relu, bias=minus_floor[:]
+            )
+
+        def invert_norm(t):
             inverse_norms[t] = norm_pool.tile([P, 1], F32, name="inverse_norm", tag="inverse_norm")
-            nc.vector.tensor_scalar_min(out=inverse_norms[t][:], in0=roots[t][:], scalar1=1.0 / EPS)
+            nc.scalar.activation(
+                out=inverse_norms[t][:], in_=excess[t][:], func=ACT.Abs_reciprocal_sqrt, bias=floor[:]
+            )
 
         def value_chunk(t, c):
             tokens = slice(t * P, (t + 1) * P)
@@ -243,17 +251,18 @@ def tile_hydraencoderlayer_pa_kernel(tc, x, wk, wv, out):
             return 0 <= t < TILES
 
         def vector_key_chunks(t):
-            return range(0) if t < 4 else range(1)
+            return range(0) if t < 6 else range(2)
 
         def values_done(t):
             return max(0, min(t, TILES, 2 * t - 5))
 
         wk_grouped = [None] * CHUNKS
         wv_grouped = [None] * CHUNKS
-        x_first = regroup_x(0, 1, v_copy)
+        x_grouped = {}
+        x_grouped[0] = regroup_x(0, 1, v_copy)
         wk_grouped[1] = regroup_weight_chunk(wk_raw[1], s_copy)
         wk_grouped[0] = regroup_weight_chunk(wk_raw[0], v_copy)
-        quantise_x(x_first, 0, 1)
+        quantise_x(x_grouped[0], 0, 1)
         quantise_weight_chunk(wk_grouped[0], wk_codes, wk_scales, 0)
         key_chunk(0, 0, False)
         wk_grouped[2] = regroup_weight_chunk(wk_raw[2], v_copy)
@@ -264,31 +273,43 @@ def tile_hydraencoderlayer_pa_kernel(tc, x, wk, wv, out):
             quantise_weight_chunk(wk_grouped[c], wk_codes, wk_scales, c)
             key_chunk(0, c, False)
         sum_of_squares(0)
-        x_second = regroup_x(1, 1, v_copy)
-        grouped_x = regroup_x(2, 2, v_copy)
-        quantise_x(x_second, 1, 1)
-        quantise_x(grouped_x, 2, 2)
+        x_grouped[1] = regroup_x(1, 1, v_copy)
+        x_grouped[2] = regroup_x(2, 2, v_copy)
+        quantise_x(x_grouped[1], 1, 1)
+        quantise_x(x_grouped[2], 2, 2)
+
+        def scalar_stage(t):
+            own = [c for c in range(CHUNKS) if c not in vector_key_chunks(t)]
+            for n in range(len(own)):
+                key_chunk(t, own[n], False)
+                if n == 0:
+                    limit_norm(t - 1)
+                if n == 1:
+                    invert_norm(t - 1)
+            sum_of_squares(t)
+
+        scalar_stage(1)
         wv_grouped[0] = regroup_weight_chunk(wv_raw[0], v_copy)
         wv_grouped[1] = regroup_weight_chunk(wv_raw[1], v_copy)
-        grouped_x = regroup_x(4, 2, v_copy)
         quantise_weight_chunk(wv_grouped[0], wv_codes, wv_scales, 0)
         wv_grouped[2] = regroup_weight_chunk(wv_raw[2], v_copy)
         quantise_weight_chunk(wv_grouped[1], wv_codes, wv_scales, 1)
+        scalar_stage(2)
         wv_grouped[3] = regroup_weight_chunk(wv_raw[3], v_copy)
         quantise_weight_chunk(wv_grouped[2], wv_codes, wv_scales, 2)
-        quantise_x(grouped_x, 4, 2)
+        x_grouped[4] = regroup_x(4, 2, v_copy)
         quantise_weight_chunk(wv_grouped[3], wv_codes, wv_scales, 3)
+        for first in range(6, TILES, 2):
+            x_grouped[first] = regroup_x(first, 2, v_copy)
+            quantise_x(x_grouped[first - 2], first - 2, 2)
+        quantise_x(x_grouped[TILES - 2], TILES - 2, 2)
 
-        for t in range(1, TILES + 1):
+        for t in range(3, TILES + 1):
             if is_tile(t):
-                for c in range(CHUNKS):
-                    if c not in vector_key_chunks(t):
-                        key_chunk(t, c, False)
-                    if c == vector_key_chunks(t).stop:
-                        root_norm(t - 1)
-                sum_of_squares(t)
+                scalar_stage(t)
             else:
-                root_norm(t - 1)
+                limit_norm(t - 1)
+                invert_norm(t - 1)
             first_group_chunk = t - FIRST_GROUP_SUM
             summing = 0 <= first_group_chunk < CHUNKS
             if is_tile(t + 1):
@@ -296,18 +317,13 @@ def tile_hydraencoderlayer_pa_kernel(tc, x, wk, wv, out):
                     key_chunk(t + 1, c, True)
             if summing:
                 turned = turn_and_add(0, first_group_chunk, vector_banks)
-            if t % 2 == 0 and is_tile(t + 4):
-                grouped_x = regroup_x(t + 4, 2, v_copy)
             for v in range(values_done(t - 1), values_done(t)):
-                limit_norm(v)
                 for c in range(CHUNKS):
                     value_chunk(v, c)
                     add_product(v, c)
                     if c > 0 and v == TILES - 1:
                         turned = turn_and_add(1, c - 1, scalar_banks)
                         sum_over_tokens(1, c - 1, turned)
-            if t % 2 == 1 and t > 1 and is_tile(t + 3):
-                quantise_x(grouped_x, t + 3, 2)
             if summing:
                 sum_over_tokens(0, first_group_chunk, turned)
         turned = turn_and_add(1, CHUNKS - 1, scalar_banks)

@@ -205,9 +205,9 @@ def tile_hydraencoderlayer_pa_kernel(tc, x, wk, wv, out):
             )
             nc.vector.scalar_tensor_tensor(
                 out=products[t][:, columns],
-                in0=v_bank[:],
+                in0=keys[t][:, columns],
                 scalar=inverse_norms[t][:],
-                in1=keys[t][:, columns],
+                in1=v_bank[:],
                 op0=ALU.mult,
                 op1=ALU.mult,
             )

@@ -29,8 +29,9 @@ GROUPS = (
     ((0, 1), (2, 3), (4, 5), (6, 7)),
     ((8, 9, 10, 11, 12, 13), (14,), (15,)),
 )
+LAST_GROUP = len(GROUPS) - 1
 LAST_ADDED = 14
-FIRST_GROUP_SUM = 11
+SUM_TIMES = ((11, 1),)
 
 FLOPS = 2 * 2 * BATCHES * TOKENS * FEATURES * WIDTH
 
@@ -43,10 +44,10 @@ def tile_hydraencoderlayer_pa_kernel(tc, x, wk, wv, out):
         raw_pool = ctx.enter_context(tc.tile_pool(name="raw", bufs=2 * CHUNKS))
         grouped_pool = ctx.enter_context(tc.tile_pool(name="grouped", bufs=4))
         key_pool = ctx.enter_context(tc.tile_pool(name="keys", bufs=VALUE_LAG + 2))
-        square_pool = ctx.enter_context(tc.tile_pool(name="squares", bufs=2))
+        square_pool = ctx.enter_context(tc.tile_pool(name="squares", bufs=1))
         norm_pool = ctx.enter_context(tc.tile_pool(name="norms", bufs=VALUE_LAG + 2))
         product_pool = ctx.enter_context(tc.tile_pool(name="products", bufs=2))
-        addend_pool = ctx.enter_context(tc.tile_pool(name="addends", bufs=6))
+        addend_pool = ctx.enter_context(tc.tile_pool(name="addends", bufs=7))
         scalar_banks = ctx.enter_context(tc.psum_pool(name="scalar_banks", bufs=4))
         vector_banks = ctx.enter_context(tc.psum_pool(name="vector_banks", bufs=4))
 
@@ -92,10 +93,15 @@ def tile_hydraencoderlayer_pa_kernel(tc, x, wk, wv, out):
         wv_codes = keep.tile([P, WIDTH], U32, align_bytes=64)
         wv_scales = keep.tile([P, WIDTH], U8, align_bytes=64)
 
-        def regroup_x(first, count, copy):
-            grouped = grouped_pool.tile([P, 2 * P, PACK], BF16, tag="x_grouped", bufs=3, align_bytes=64)
+        ones = keep.tile([P, CHUNK], BF16)
+        nc.gpsimd.memset(ones[:], 1.0)
+
+        def keep_warm(bank, count):
+            for n in range(count):
+                nc.tensor.matmul(out=bank, lhsT=ones[:, 0:P], rhs=ones[:], start=True, stop=True)
+
+        def turn_x(first, count):
             x_words = x_raw[:].bitcast(F32)
-            grouped_words = grouped[:].bitcast(F32)
             flipped = vector_banks.tile([P, 2, 2, P], F32, tag="bank")
             for n in range(count):
                 for u in range(2):
@@ -104,6 +110,11 @@ def tile_hydraencoderlayer_pa_kernel(tc, x, wk, wv, out):
                         x_words[:, first + n, u : FEATURES // 2 : 2],
                         identity[:],
                     )
+            return flipped
+
+        def regroup_x(flipped, count, copy):
+            grouped = grouped_pool.tile([P, 2 * P, PACK], BF16, tag="x_grouped", bufs=3, align_bytes=64)
+            grouped_words = grouped[:].bitcast(F32)
             copy(
                 out=grouped_words[:, 0 : count * P, :].rearrange("p (n k) u -> p n k u", n=count),
                 in_=flipped[:, 0:count].rearrange("p n u k -> p n k u"),
@@ -194,6 +205,8 @@ def tile_hydraencoderlayer_pa_kernel(tc, x, wk, wv, out):
                 else:
                     products[t] = product_pool.tile([P, WIDTH], F32, name="product", tag="product")
             v_bank = vector_banks.tile([P, CHUNK], F32, tag="bank")
+            if t == TILES - 1:
+                keep_warm(v_bank[:], 2)
             nc.tensor.matmul_mx(
                 out=v_bank[:],
                 lhsT=x_codes[:, tokens].bitcast(FP8X4),
@@ -256,28 +269,6 @@ def tile_hydraencoderlayer_pa_kernel(tc, x, wk, wv, out):
         def values_done(t):
             return max(0, min(t, TILES, 2 * t - 5))
 
-        wk_grouped = [None] * CHUNKS
-        wv_grouped = [None] * CHUNKS
-        x_grouped = {}
-        x_grouped[0] = regroup_x(0, 1, v_copy)
-        wk_grouped[1] = regroup_weight_chunk(wk_raw[1], s_copy)
-        wk_grouped[0] = regroup_weight_chunk(wk_raw[0], v_copy)
-        quantise_x(x_grouped[0], 0, 1)
-        quantise_weight_chunk(wk_grouped[0], wk_codes, wk_scales, 0)
-        key_chunk(0, 0, False)
-        wk_grouped[2] = regroup_weight_chunk(wk_raw[2], v_copy)
-        quantise_weight_chunk(wk_grouped[1], wk_codes, wk_scales, 1)
-        key_chunk(0, 1, False)
-        wk_grouped[3] = regroup_weight_chunk(wk_raw[3], v_copy)
-        for c in range(2, CHUNKS):
-            quantise_weight_chunk(wk_grouped[c], wk_codes, wk_scales, c)
-            key_chunk(0, c, False)
-        sum_of_squares(0)
-        x_grouped[1] = regroup_x(1, 1, v_copy)
-        x_grouped[2] = regroup_x(2, 2, v_copy)
-        quantise_x(x_grouped[1], 1, 1)
-        quantise_x(x_grouped[2], 2, 2)
-
         def scalar_stage(t):
             own = [c for c in range(CHUNKS) if c not in vector_key_chunks(t)]
             for n in range(len(own)):
@@ -288,19 +279,50 @@ def tile_hydraencoderlayer_pa_kernel(tc, x, wk, wv, out):
                     invert_norm(t - 1)
             sum_of_squares(t)
 
+        wk_grouped = [None] * CHUNKS
+        wv_grouped = [None] * CHUNKS
+        x_turned = {}
+        x_grouped = {}
+        x_turned[0] = turn_x(0, 1)
+        x_grouped[0] = regroup_x(x_turned[0], 1, v_copy)
+        wk_grouped[1] = regroup_weight_chunk(wk_raw[1], s_copy)
+        wk_grouped[0] = regroup_weight_chunk(wk_raw[0], v_copy)
+        quantise_x(x_grouped[0], 0, 1)
+        quantise_weight_chunk(wk_grouped[0], wk_codes, wk_scales, 0)
+        key_chunk(0, 0, False)
+        wk_grouped[2] = regroup_weight_chunk(wk_raw[2], v_copy)
+        quantise_weight_chunk(wk_grouped[1], wk_codes, wk_scales, 1)
+        key_chunk(0, 1, False)
+        wk_grouped[3] = regroup_weight_chunk(wk_raw[3], v_copy)
+        quantise_weight_chunk(wk_grouped[2], wk_codes, wk_scales, 2)
+        key_chunk(0, 2, False)
+        x_turned[1] = turn_x(1, 1)
+        quantise_weight_chunk(wk_grouped[3], wk_codes, wk_scales, 3)
+        key_chunk(0, 3, False)
+        x_turned[2] = turn_x(2, 2)
+        sum_of_squares(0)
+        x_grouped[1] = regroup_x(x_turned[1], 1, v_copy)
+        x_grouped[2] = regroup_x(x_turned[2], 2, v_copy)
+        quantise_x(x_grouped[1], 1, 1)
+        quantise_x(x_grouped[2], 2, 2)
+
         scalar_stage(1)
+        x_turned[4] = turn_x(4, 2)
         wv_grouped[0] = regroup_weight_chunk(wv_raw[0], v_copy)
         wv_grouped[1] = regroup_weight_chunk(wv_raw[1], v_copy)
         quantise_weight_chunk(wv_grouped[0], wv_codes, wv_scales, 0)
         wv_grouped[2] = regroup_weight_chunk(wv_raw[2], v_copy)
         quantise_weight_chunk(wv_grouped[1], wv_codes, wv_scales, 1)
         scalar_stage(2)
+        x_turned[6] = turn_x(6, 2)
         wv_grouped[3] = regroup_weight_chunk(wv_raw[3], v_copy)
         quantise_weight_chunk(wv_grouped[2], wv_codes, wv_scales, 2)
-        x_grouped[4] = regroup_x(4, 2, v_copy)
+        x_grouped[4] = regroup_x(x_turned[4], 2, v_copy)
         quantise_weight_chunk(wv_grouped[3], wv_codes, wv_scales, 3)
         for first in range(6, TILES, 2):
-            x_grouped[first] = regroup_x(first, 2, v_copy)
+            if first + 2 < TILES:
+                x_turned[first + 2] = turn_x(first + 2, 2)
+            x_grouped[first] = regroup_x(x_turned[first], 2, v_copy)
             quantise_x(x_grouped[first - 2], first - 2, 2)
         quantise_x(x_grouped[TILES - 2], TILES - 2, 2)
 
@@ -310,24 +332,31 @@ def tile_hydraencoderlayer_pa_kernel(tc, x, wk, wv, out):
             else:
                 limit_norm(t - 1)
                 invert_norm(t - 1)
-            first_group_chunk = t - FIRST_GROUP_SUM
-            summing = 0 <= first_group_chunk < CHUNKS
+            due = []
+            for g in range(LAST_GROUP):
+                first, count = SUM_TIMES[g]
+                for c in range((t - first) * count, (t - first + 1) * count):
+                    if 0 <= c < CHUNKS:
+                        due.append((g, c))
             if is_tile(t + 1):
                 for c in vector_key_chunks(t + 1):
                     key_chunk(t + 1, c, True)
-            if summing:
-                turned = turn_and_add(0, first_group_chunk, vector_banks)
+            if t == TILES:
+                for n in range(len(due)):
+                    sum_over_tokens(due[n][0], due[n][1], turn_and_add(due[n][0], due[n][1], vector_banks))
             for v in range(values_done(t - 1), values_done(t)):
                 for c in range(CHUNKS):
                     value_chunk(v, c)
                     add_product(v, c)
-                    if c > 0 and v == TILES - 1:
-                        turned = turn_and_add(1, c - 1, scalar_banks)
-                        sum_over_tokens(1, c - 1, turned)
-            if summing:
-                sum_over_tokens(0, first_group_chunk, turned)
-        turned = turn_and_add(1, CHUNKS - 1, scalar_banks)
-        sum_over_tokens(1, CHUNKS - 1, turned)
+                    if v == TILES - 1:
+                        if c > 0:
+                            last = turn_and_add(LAST_GROUP, c - 1, scalar_banks)
+                            sum_over_tokens(LAST_GROUP, c - 1, last)
+            if t < TILES:
+                for n in range(len(due)):
+                    sum_over_tokens(due[n][0], due[n][1], turn_and_add(due[n][0], due[n][1], vector_banks))
+        last = turn_and_add(LAST_GROUP, CHUNKS - 1, scalar_banks)
+        sum_over_tokens(LAST_GROUP, CHUNKS - 1, last)
 
         rows = BATCHES * CHUNKS * BLOCKS
         turned_sums = scalar_banks.tile([P, P], F32, tag="bank")

@@ -26,12 +26,12 @@ TILES = BATCHES * TOKENS // P
 VALUE_LAG = 3
 
 GROUPS = (
-    ((0, 1), (2, 3), (4, 5), (6, 7)),
-    ((8, 9, 10, 11, 12, 13), (14,), (15,)),
+    ((0, 1, 2), (3, 4, 5), (6, 7, 8)),
+    ((9, 10, 11, 12), (13, 14), (15,)),
 )
 LAST_GROUP = len(GROUPS) - 1
 LAST_ADDED = 14
-SUM_TIMES = ((11, 1),)
+SUM_TIMES = ((12, 1),)
 
 FLOPS = 2 * 2 * BATCHES * TOKENS * FEATURES * WIDTH
 
@@ -47,7 +47,7 @@ def tile_hydraencoderlayer_pa_kernel(tc, x, wk, wv, out):
         square_pool = ctx.enter_context(tc.tile_pool(name="squares", bufs=1))
         norm_pool = ctx.enter_context(tc.tile_pool(name="norms", bufs=VALUE_LAG + 2))
         product_pool = ctx.enter_context(tc.tile_pool(name="products", bufs=2))
-        addend_pool = ctx.enter_context(tc.tile_pool(name="addends", bufs=7))
+        addend_pool = ctx.enter_context(tc.tile_pool(name="addends", bufs=8))
         scalar_banks = ctx.enter_context(tc.psum_pool(name="scalar_banks", bufs=4))
         vector_banks = ctx.enter_context(tc.psum_pool(name="vector_banks", bufs=4))
 
@@ -67,8 +67,9 @@ def tile_hydraencoderlayer_pa_kernel(tc, x, wk, wv, out):
             return raw
 
         load_x(0, 1)
-        wk_raw = [load_weight_chunk(wk, c) for c in range(CHUNKS)]
+        wk_raw = [load_weight_chunk(wk, c) for c in range(3)]
         load_x(1, 3)
+        wk_raw.append(load_weight_chunk(wk, 3))
         wv_raw = [load_weight_chunk(wv, c) for c in range(CHUNKS)]
         for first in range(4, TILES, 4):
             load_x(first, 4)
@@ -158,7 +159,9 @@ def tile_hydraencoderlayer_pa_kernel(tc, x, wk, wv, out):
                 for t in members:
                     addend_of[t] = members
 
-        def key_chunk(t, c, on_vector):
+        a_banks = {}
+
+        def key_pass(t, c, on_vector):
             tokens = slice(t * P, (t + 1) * P)
             columns = slice(c * CHUNK, (c + 1) * CHUNK)
             if keys[t] is None:
@@ -174,7 +177,15 @@ def tile_hydraencoderlayer_pa_kernel(tc, x, wk, wv, out):
                 start=True,
                 stop=True,
             )
-            copy(out=keys[t][:, columns], in_=a_bank[:])
+            a_banks[t, c] = (a_bank, copy)
+
+        def key_copy(t, c):
+            a_bank, copy = a_banks[t, c]
+            copy(out=keys[t][:, c * CHUNK : (c + 1) * CHUNK], in_=a_bank[:])
+
+        def key_chunk(t, c, on_vector):
+            key_pass(t, c, on_vector)
+            key_copy(t, c)
 
         def sum_of_squares(t):
             squares = square_pool.tile([P, WIDTH], BF16, tag="squares")
@@ -264,15 +275,20 @@ def tile_hydraencoderlayer_pa_kernel(tc, x, wk, wv, out):
             return 0 <= t < TILES
 
         def vector_key_chunks(t):
-            return range(0) if t < 6 else range(2)
+            return range(0) if t < 5 else range(2)
 
         def values_done(t):
             return max(0, min(t, TILES, 2 * t - 5))
 
+        def scalar_chunks(t):
+            return [c for c in range(CHUNKS) if c not in vector_key_chunks(t)]
+
         def scalar_stage(t):
-            own = [c for c in range(CHUNKS) if c not in vector_key_chunks(t)]
+            own = scalar_chunks(t)
             for n in range(len(own)):
-                key_chunk(t, own[n], False)
+                if (t, own[n]) not in a_banks:
+                    key_pass(t, own[n], False)
+                key_copy(t, own[n])
                 if n == 0:
                     limit_norm(t - 1)
                 if n == 1:
@@ -290,20 +306,20 @@ def tile_hydraencoderlayer_pa_kernel(tc, x, wk, wv, out):
         quantise_x(x_grouped[0], 0, 1)
         quantise_weight_chunk(wk_grouped[0], wk_codes, wk_scales, 0)
         key_chunk(0, 0, False)
+        x_turned[1] = turn_x(1, 1)
+        x_turned[2] = turn_x(2, 2)
+        x_grouped[1] = regroup_x(x_turned[1], 1, s_copy)
+        x_grouped[2] = regroup_x(x_turned[2], 2, s_copy)
         wk_grouped[2] = regroup_weight_chunk(wk_raw[2], v_copy)
         quantise_weight_chunk(wk_grouped[1], wk_codes, wk_scales, 1)
         key_chunk(0, 1, False)
         wk_grouped[3] = regroup_weight_chunk(wk_raw[3], v_copy)
         quantise_weight_chunk(wk_grouped[2], wk_codes, wk_scales, 2)
         key_chunk(0, 2, False)
-        x_turned[1] = turn_x(1, 1)
+        quantise_x(x_grouped[1], 1, 1)
         quantise_weight_chunk(wk_grouped[3], wk_codes, wk_scales, 3)
         key_chunk(0, 3, False)
-        x_turned[2] = turn_x(2, 2)
         sum_of_squares(0)
-        x_grouped[1] = regroup_x(x_turned[1], 1, v_copy)
-        x_grouped[2] = regroup_x(x_turned[2], 2, v_copy)
-        quantise_x(x_grouped[1], 1, 1)
         quantise_x(x_grouped[2], 2, 2)
 
         scalar_stage(1)
@@ -352,6 +368,9 @@ def tile_hydraencoderlayer_pa_kernel(tc, x, wk, wv, out):
                         if c > 0:
                             last = turn_and_add(LAST_GROUP, c - 1, scalar_banks)
                             sum_over_tokens(LAST_GROUP, c - 1, last)
+            if is_tile(t + 1):
+                for c in scalar_chunks(t + 1):
+                    key_pass(t + 1, c, False)
             if t < TILES:
                 for n in range(len(due)):
                     sum_over_tokens(due[n][0], due[n][1], turn_and_add(due[n][0], due[n][1], vector_banks))

@@ -94,13 +94,6 @@ def tile_hydraencoderlayer_pa_kernel(tc, x, wk, wv, out):
         wv_codes = keep.tile([P, WIDTH], U32, align_bytes=64)
         wv_scales = keep.tile([P, WIDTH], U8, align_bytes=64)
 
-        ones = keep.tile([P, CHUNK], BF16)
-        nc.gpsimd.memset(ones[:], 1.0)
-
-        def keep_warm(bank, count):
-            for n in range(count):
-                nc.tensor.matmul(out=bank, lhsT=ones[:, 0:P], rhs=ones[:], start=True, stop=True)
-
         def turn_x(first, count):
             x_words = x_raw[:].bitcast(F32)
             flipped = vector_banks.tile([P, 2, 2, P], F32, tag="bank")
@@ -206,18 +199,12 @@ def tile_hydraencoderlayer_pa_kernel(tc, x, wk, wv, out):
                 out=inverse_norms[t][:], in_=excess[t][:], func=ACT.Abs_reciprocal_sqrt, bias=floor[:]
             )
 
-        def value_chunk(t, c):
+        v_banks = {}
+
+        def value_pass(t, c):
             tokens = slice(t * P, (t + 1) * P)
             columns = slice(c * CHUNK, (c + 1) * CHUNK)
-            members = addend_of[t]
-            if c == 0:
-                if t == members[0]:
-                    products[t] = addend_pool.tile([P, WIDTH], F32, name="addend", tag="addend")
-                else:
-                    products[t] = product_pool.tile([P, WIDTH], F32, name="product", tag="product")
-            v_bank = vector_banks.tile([P, CHUNK], F32, tag="bank")
-            if t == TILES - 1:
-                keep_warm(v_bank[:], 2)
+            v_bank = vector_banks.tile([P, CHUNK], F32, name="v_bank", tag="bank")
             nc.tensor.matmul_mx(
                 out=v_bank[:],
                 lhsT=x_codes[:, tokens].bitcast(FP8X4),
@@ -227,17 +214,27 @@ def tile_hydraencoderlayer_pa_kernel(tc, x, wk, wv, out):
                 start=True,
                 stop=True,
             )
+            v_banks[t, c] = v_bank
+
+        def product_chunk(t, c):
+            columns = slice(c * CHUNK, (c + 1) * CHUNK)
+            members = addend_of[t]
+            if c == 0:
+                if t == members[0]:
+                    products[t] = addend_pool.tile([P, WIDTH], F32, name="addend", tag="addend")
+                else:
+                    products[t] = product_pool.tile([P, WIDTH], F32, name="product", tag="product")
             nc.vector.scalar_tensor_tensor(
                 out=products[t][:, columns],
                 in0=keys[t][:, columns],
                 scalar=inverse_norms[t][:],
-                in1=v_bank[:],
+                in1=v_banks[t, c][:],
                 op0=ALU.mult,
                 op1=ALU.mult,
             )
 
         def add_product(t, c):
-            step = 1 if t >= LAST_ADDED else 2
+            step = 1 if t >= LAST_ADDED else CHUNKS
             members = addend_of[t]
             if t != members[0] and c % step == step - 1:
                 columns = slice((c + 1 - step) * CHUNK, (c + 1) * CHUNK)
@@ -278,7 +275,7 @@ def tile_hydraencoderlayer_pa_kernel(tc, x, wk, wv, out):
             return range(0) if t < 5 else range(2)
 
         def values_done(t):
-            return max(0, min(t, TILES, 2 * t - 5))
+            return max(0, min(t, TILES, 2 * t - 4))
 
         def scalar_chunks(t):
             return [c for c in range(CHUNKS) if c not in vector_key_chunks(t)]
@@ -342,6 +339,7 @@ def tile_hydraencoderlayer_pa_kernel(tc, x, wk, wv, out):
             quantise_x(x_grouped[first - 2], first - 2, 2)
         quantise_x(x_grouped[TILES - 2], TILES - 2, 2)
 
+        last_turned = []
         for t in range(3, TILES + 1):
             if is_tile(t):
                 scalar_stage(t)
@@ -361,21 +359,26 @@ def tile_hydraencoderlayer_pa_kernel(tc, x, wk, wv, out):
                 for n in range(len(due)):
                     sum_over_tokens(due[n][0], due[n][1], turn_and_add(due[n][0], due[n][1], vector_banks))
             for v in range(values_done(t - 1), values_done(t)):
+                if v == TILES - 1:
+                    for c in range(CHUNKS):
+                        value_pass(v, c)
+                    for c in range(CHUNKS):
+                        product_chunk(v, c)
+                        add_product(v, c)
+                        last_turned.append(turn_and_add(LAST_GROUP, c, scalar_banks))
+                    continue
                 for c in range(CHUNKS):
-                    value_chunk(v, c)
+                    value_pass(v, c)
+                    product_chunk(v, c)
                     add_product(v, c)
-                    if v == TILES - 1:
-                        if c > 0:
-                            last = turn_and_add(LAST_GROUP, c - 1, scalar_banks)
-                            sum_over_tokens(LAST_GROUP, c - 1, last)
             if is_tile(t + 1):
                 for c in scalar_chunks(t + 1):
                     key_pass(t + 1, c, False)
             if t < TILES:
                 for n in range(len(due)):
                     sum_over_tokens(due[n][0], due[n][1], turn_and_add(due[n][0], due[n][1], vector_banks))
-        last = turn_and_add(LAST_GROUP, CHUNKS - 1, scalar_banks)
-        sum_over_tokens(LAST_GROUP, CHUNKS - 1, last)
+        for c in range(CHUNKS):
+            sum_over_tokens(LAST_GROUP, c, last_turned[c])
 
         rows = BATCHES * CHUNKS * BLOCKS
         turned_sums = scalar_banks.tile([P, P], F32, tag="bank")

@@ -182,21 +182,42 @@ def tile_hydraencoderlayer_pa_kernel(tc, x, wk, wv, out):
 
         def sum_of_squares(t):
             squares = square_pool.tile([P, WIDTH], BF16, tag="squares")
-            norms_squared[t] = norm_pool.tile([P, 1], F32, name="norm_squared", tag="norm_squared")
+            first, count = norm_group(t)
+            if t == first:
+                norms_squared[t] = norm_pool.tile([P, 2], F32, name="norms_squared", tag="norms_squared")
+            place = t - first
             nc.scalar.activation(
-                out=squares[:], in_=keys[t][:], func=ACT.Square, accum_out=norms_squared[t][:]
+                out=squares[:],
+                in_=keys[t][:],
+                func=ACT.Square,
+                accum_out=norms_squared[first][:, place : place + 1],
             )
 
+        def norm_group(t):
+            return (t - t % 2, 2) if t < 4 else (t, 1)
+
         def limit_norm(t):
-            excess[t] = norm_pool.tile([P, 1], F32, name="excess", tag="excess")
+            first, count = norm_group(t)
+            if t != first + count - 1:
+                return
+            excess[first] = norm_pool.tile([P, 2], F32, name="excess", tag="excess")
             nc.scalar.activation(
-                out=excess[t][:], in_=norms_squared[t][:], func=ACT.Relu, bias=minus_floor[:]
+                out=excess[first][:, 0:count],
+                in_=norms_squared[first][:, 0:count],
+                func=ACT.Relu,
+                bias=minus_floor[:],
             )
 
         def invert_norm(t):
-            inverse_norms[t] = norm_pool.tile([P, 1], F32, name="inverse_norm", tag="inverse_norm")
+            first, count = norm_group(t)
+            if t != first + count - 1:
+                return
+            inverse_norms[first] = norm_pool.tile([P, 2], F32, name="inverse_norms", tag="inverse_norms")
             nc.scalar.activation(
-                out=inverse_norms[t][:], in_=excess[t][:], func=ACT.Abs_reciprocal_sqrt, bias=floor[:]
+                out=inverse_norms[first][:, 0:count],
+                in_=excess[first][:, 0:count],
+                func=ACT.Abs_reciprocal_sqrt,
+                bias=floor[:],
             )
 
         v_banks = {}
@@ -224,10 +245,11 @@ def tile_hydraencoderlayer_pa_kernel(tc, x, wk, wv, out):
                     products[t] = addend_pool.tile([P, WIDTH], F32, name="addend", tag="addend")
                 else:
                     products[t] = product_pool.tile([P, WIDTH], F32, name="product", tag="product")
+            first, count = norm_group(t)
             nc.vector.scalar_tensor_tensor(
                 out=products[t][:, columns],
                 in0=keys[t][:, columns],
-                scalar=inverse_norms[t][:],
+                scalar=inverse_norms[first][:, t - first : t - first + 1],
                 in1=v_banks[t, c][:],
                 op0=ALU.mult,
                 op1=ALU.mult,

@@ -27,10 +27,12 @@ VALUE_LAG = 3
 
 GROUPS = (
     ((0, 1, 2), (3, 4, 5), (6, 7, 8)),
-    ((9, 10, 11, 12), (13, 14), (15,)),
+    ((9, 10, 11), (12, 13), (14,), (15,)),
 )
 LAST_GROUP = len(GROUPS) - 1
-LAST_ADDED = 14
+LAST_ADDED = 16
+EARLY = 1
+VK = {5: 2, 6: 2, 7: 2, 8: 2, 9: 2, 10: 2, 11: 2, 12: 2, 13: 2, 14: 2, 15: 2}
 SUM_TIMES = ((12, 1),)
 
 FLOPS = 2 * 2 * BATCHES * TOKENS * FEATURES * WIDTH
@@ -47,7 +49,7 @@ def tile_hydraencoderlayer_pa_kernel(tc, x, wk, wv, out):
         square_pool = ctx.enter_context(tc.tile_pool(name="squares", bufs=1))
         norm_pool = ctx.enter_context(tc.tile_pool(name="norms", bufs=VALUE_LAG + 2))
         product_pool = ctx.enter_context(tc.tile_pool(name="products", bufs=2))
-        addend_pool = ctx.enter_context(tc.tile_pool(name="addends", bufs=8))
+        addend_pool = ctx.enter_context(tc.tile_pool(name="addends", bufs=7))
         scalar_banks = ctx.enter_context(tc.psum_pool(name="scalar_banks", bufs=4))
         vector_banks = ctx.enter_context(tc.psum_pool(name="vector_banks", bufs=4))
 
@@ -265,6 +267,25 @@ def tile_hydraencoderlayer_pa_kernel(tc, x, wk, wv, out):
                     out=addend, in0=addend, in1=products[t][:, columns], op=ALU.add
                 )
 
+        def turn_addends(g, c, banks, first, last):
+            addends = GROUPS[g]
+            if first == 0:
+                turned_of[g, c] = banks.tile([P, BLOCKS, P], F32, name="turned", tag="bank")
+            turned = turned_of[g, c]
+            for n in range(first, last):
+                for j in range(BLOCKS):
+                    nc.tensor.matmul(
+                        out=turned[:, j, :],
+                        lhsT=products[addends[n][0]][:, c * CHUNK + j * P : c * CHUNK + (j + 1) * P],
+                        rhs=identity[:],
+                        is_transpose=True,
+                        start=n == 0 and j == 0,
+                        stop=n == len(addends) - 1 and j == BLOCKS - 1,
+                    )
+            return turned
+
+        turned_of = {}
+
         def turn_and_add(g, c, banks):
             turned = banks.tile([P, BLOCKS, P], F32, name="turned", tag="bank")
             addends = GROUPS[g]
@@ -294,7 +315,7 @@ def tile_hydraencoderlayer_pa_kernel(tc, x, wk, wv, out):
             return 0 <= t < TILES
 
         def vector_key_chunks(t):
-            return range(0) if t < 5 else range(2)
+            return range(VK.get(t, 0))
 
         def values_done(t):
             return max(0, min(t, TILES, 2 * t - 4))
@@ -386,8 +407,20 @@ def tile_hydraencoderlayer_pa_kernel(tc, x, wk, wv, out):
                         value_pass(v, c)
                     for c in range(CHUNKS):
                         product_chunk(v, c)
+                        last_turned.append(
+                            turn_addends(LAST_GROUP, c, scalar_banks, EARLY, len(GROUPS[LAST_GROUP]))
+                        )
+                        if c > 0:
+                            sum_over_tokens(LAST_GROUP, c - 1, last_turned[c - 1])
+                    continue
+                if v == TILES - 2:
+                    for c in range(CHUNKS):
+                        value_pass(v, c)
+                    for c in range(CHUNKS):
+                        turn_addends(LAST_GROUP, c, scalar_banks, 0, EARLY)
+                    for c in range(CHUNKS):
+                        product_chunk(v, c)
                         add_product(v, c)
-                        last_turned.append(turn_and_add(LAST_GROUP, c, scalar_banks))
                     continue
                 for c in range(CHUNKS):
                     value_pass(v, c)
@@ -399,8 +432,7 @@ def tile_hydraencoderlayer_pa_kernel(tc, x, wk, wv, out):
             if t < TILES:
                 for n in range(len(due)):
                     sum_over_tokens(due[n][0], due[n][1], turn_and_add(due[n][0], due[n][1], vector_banks))
-        for c in range(CHUNKS):
-            sum_over_tokens(LAST_GROUP, c, last_turned[c])
+        sum_over_tokens(LAST_GROUP, CHUNKS - 1, last_turned[CHUNKS - 1])
 
         rows = BATCHES * CHUNKS * BLOCKS
         turned_sums = scalar_banks.tile([P, P], F32, tag="bank")

@@ -27,13 +27,13 @@ VALUE_LAG = 3
 
 GROUPS = (
     ((0, 1, 2), (3, 4, 5), (6, 7, 8)),
-    ((9, 10, 11), (12, 13), (14,), (15,)),
+    ((9, 10), (11, 12), (13, 14), (15,)),
 )
 LAST_GROUP = len(GROUPS) - 1
-LAST_ADDED = 16
+LAST_ADDED = 14
 EARLY = 1
 VK = {5: 2, 6: 2, 7: 2, 8: 2, 9: 2, 10: 2, 11: 2, 12: 2, 13: 2, 14: 2, 15: 2}
-SUM_TIMES = ((12, 1),)
+SUM_TIMES = ((11, 1),)
 
 FLOPS = 2 * 2 * BATCHES * TOKENS * FEATURES * WIDTH
 

@@ -23,16 +23,21 @@ CHUNK = 512
 CHUNKS = WIDTH // CHUNK
 BLOCKS = CHUNK // P
 TILES = BATCHES * TOKENS // P
-VALUE_LAG = 3
+KEYS = 6
 
 GROUPS = (
     ((0, 1, 2), (3, 4, 5), (6, 7, 8)),
-    ((9, 10), (11, 12), (13, 14), (15,)),
+    ((9, 10, 11, 12), (13, 14), (15,)),
 )
 LAST_GROUP = len(GROUPS) - 1
 LAST_ADDED = 14
 EARLY = 1
-VK = {5: 2, 6: 2, 7: 2, 8: 2, 9: 2, 10: 2, 11: 2, 12: 2, 13: 2, 14: 2, 15: 2}
+WVL = (2, 2)
+RAWB = {1: 4, 2: 2}
+VK = {5: 1, 6: 2, 7: 2, 8: 2, 9: 2, 10: 2, 11: 2, 12: 2, 13: 2, 14: 2, 15: 2}
+FIRSTV = 6
+KPC = 3
+EARLY_TILES = 4
 SUM_TIMES = ((11, 1),)
 
 FLOPS = 2 * 2 * BATCHES * TOKENS * FEATURES * WIDTH
@@ -45,9 +50,9 @@ def tile_hydraencoderlayer_pa_kernel(tc, x, wk, wv, out):
         keep = ctx.enter_context(tc.tile_pool(name="keep", bufs=1))
         raw_pool = ctx.enter_context(tc.tile_pool(name="raw", bufs=2 * CHUNKS))
         grouped_pool = ctx.enter_context(tc.tile_pool(name="grouped", bufs=4))
-        key_pool = ctx.enter_context(tc.tile_pool(name="keys", bufs=VALUE_LAG + 2))
+        key_pool = ctx.enter_context(tc.tile_pool(name="keys", bufs=KEYS))
         square_pool = ctx.enter_context(tc.tile_pool(name="squares", bufs=1))
-        norm_pool = ctx.enter_context(tc.tile_pool(name="norms", bufs=VALUE_LAG + 2))
+        norm_pool = ctx.enter_context(tc.tile_pool(name="norms", bufs=KEYS))
         product_pool = ctx.enter_context(tc.tile_pool(name="products", bufs=2))
         addend_pool = ctx.enter_context(tc.tile_pool(name="addends", bufs=7))
         scalar_banks = ctx.enter_context(tc.psum_pool(name="scalar_banks", bufs=4))
@@ -60,19 +65,26 @@ def tile_hydraencoderlayer_pa_kernel(tc, x, wk, wv, out):
             tiles = slice(first, first + count)
             nc.sync.dma_start(out=x_raw[:, tiles, :], in_=x_rows[:, tiles, :])
 
-        def load_weight_chunk(w, c):
-            raw = raw_pool.tile([P, PACK, CHUNK], BF16, tag="raw")
+        def load_weight_chunks(w, first, count):
+            raw = raw_pool.tile([P, PACK, count * CHUNK], BF16, name="raw", tag="raw" + str(count), bufs=RAWB[count])
             nc.sync.dma_start(
                 out=raw[:],
-                in_=w[:, c * CHUNK : (c + 1) * CHUNK].rearrange("(p t) c -> p t c", t=PACK),
+                in_=w[:, first * CHUNK : (first + count) * CHUNK].rearrange("(p t) c -> p t c", t=PACK),
             )
-            return raw
+            return [raw[:, :, c * CHUNK : (c + 1) * CHUNK] for c in range(count)]
+
+        def load_weights(w, counts):
+            chunks = []
+            for count in counts:
+                chunks.extend(load_weight_chunks(w, len(chunks), count))
+            return chunks
 
         load_x(0, 1)
-        wk_raw = [load_weight_chunk(wk, c) for c in range(3)]
-        load_x(1, 3)
-        wk_raw.append(load_weight_chunk(wk, 3))
-        wv_raw = [load_weight_chunk(wv, c) for c in range(CHUNKS)]
+        wk_raw = load_weight_chunks(wk, 0, 1)
+        load_x(1, EARLY_TILES - 1)
+        for c in range(1, CHUNKS):
+            wk_raw.extend(load_weight_chunks(wk, c, 1))
+        wv_raw = load_weights(wv, WVL)
         for first in range(4, TILES, 4):
             load_x(first, 4)
 
@@ -129,7 +141,7 @@ def tile_hydraencoderlayer_pa_kernel(tc, x, wk, wv, out):
             grouped = grouped_pool.tile([P, CHUNK, PACK], BF16, tag="w_grouped", align_bytes=64)
             copy(
                 out=grouped[:].rearrange("p (c i) t -> p c t i", i=4),
-                in_=raw[:].rearrange("p t (c i) -> p c t i", i=4),
+                in_=raw.rearrange("p t (c i) -> p c t i", i=4),
             )
             return grouped
 
@@ -196,7 +208,7 @@ def tile_hydraencoderlayer_pa_kernel(tc, x, wk, wv, out):
             )
 
         def norm_group(t):
-            return (t - t % 2, 2) if t < 4 else (t, 1)
+            return (t, 1)
 
         def limit_norm(t):
             first, count = norm_group(t)
@@ -223,6 +235,12 @@ def tile_hydraencoderlayer_pa_kernel(tc, x, wk, wv, out):
             )
 
         v_banks = {}
+        passes = [0]
+
+        def value_passes(upto):
+            while passes[0] < min(upto, TILES * CHUNKS):
+                value_pass(passes[0] // CHUNKS, passes[0] % CHUNKS)
+                passes[0] += 1
 
         def value_pass(t, c):
             tokens = slice(t * P, (t + 1) * P)
@@ -318,7 +336,7 @@ def tile_hydraencoderlayer_pa_kernel(tc, x, wk, wv, out):
             return range(VK.get(t, 0))
 
         def values_done(t):
-            return max(0, min(t, TILES, 2 * t - 4))
+            return max(0, min(t, TILES, 2 * t - FIRSTV))
 
         def scalar_chunks(t):
             return [c for c in range(CHUNKS) if c not in vector_key_chunks(t)]
@@ -331,48 +349,49 @@ def tile_hydraencoderlayer_pa_kernel(tc, x, wk, wv, out):
                 key_copy(t, own[n])
                 if n == 0:
                     limit_norm(t - 1)
-                if n == 1:
+                if n == min(1, len(own) - 1):
                     invert_norm(t - 1)
             sum_of_squares(t)
 
-        wk_grouped = [None] * CHUNKS
         wv_grouped = [None] * CHUNKS
         x_turned = {}
         x_grouped = {}
         x_turned[0] = turn_x(0, 1)
-        x_grouped[0] = regroup_x(x_turned[0], 1, v_copy)
-        wk_grouped[1] = regroup_weight_chunk(wk_raw[1], s_copy)
-        wk_grouped[0] = regroup_weight_chunk(wk_raw[0], v_copy)
+        x_grouped[0] = regroup_x(x_turned[0], 1, s_copy)
+        wk_grouped = regroup_weight_chunk(wk_raw[0], v_copy)
         quantise_x(x_grouped[0], 0, 1)
-        quantise_weight_chunk(wk_grouped[0], wk_codes, wk_scales, 0)
-        key_chunk(0, 0, False)
+        quantise_weight_chunk(wk_grouped, wk_codes, wk_scales, 0)
         x_turned[1] = turn_x(1, 1)
         x_turned[2] = turn_x(2, 2)
+        key_pass(0, 0, False)
         x_grouped[1] = regroup_x(x_turned[1], 1, s_copy)
         x_grouped[2] = regroup_x(x_turned[2], 2, s_copy)
-        wk_grouped[2] = regroup_weight_chunk(wk_raw[2], v_copy)
-        quantise_weight_chunk(wk_grouped[1], wk_codes, wk_scales, 1)
-        key_chunk(0, 1, False)
-        wk_grouped[3] = regroup_weight_chunk(wk_raw[3], v_copy)
-        quantise_weight_chunk(wk_grouped[2], wk_codes, wk_scales, 2)
-        key_chunk(0, 2, False)
+        key_copy(0, 0)
         quantise_x(x_grouped[1], 1, 1)
-        quantise_weight_chunk(wk_grouped[3], wk_codes, wk_scales, 3)
-        key_chunk(0, 3, False)
-        sum_of_squares(0)
         quantise_x(x_grouped[2], 2, 2)
+        for c in range(1, CHUNKS):
+            wk_grouped = regroup_weight_chunk(wk_raw[c], v_copy)
+            for t in range(1, EARLY_TILES):
+                key_chunk(t, c - 1, False)
+            quantise_weight_chunk(wk_grouped, wk_codes, wk_scales, c)
+            key_chunk(0, c, False)
+        for t in range(1, EARLY_TILES):
+            key_chunk(t, CHUNKS - 1, False)
+        sum_of_squares(0)
 
-        scalar_stage(1)
-        x_turned[4] = turn_x(4, 2)
         wv_grouped[0] = regroup_weight_chunk(wv_raw[0], v_copy)
         wv_grouped[1] = regroup_weight_chunk(wv_raw[1], v_copy)
         quantise_weight_chunk(wv_grouped[0], wv_codes, wv_scales, 0)
         wv_grouped[2] = regroup_weight_chunk(wv_raw[2], v_copy)
         quantise_weight_chunk(wv_grouped[1], wv_codes, wv_scales, 1)
-        scalar_stage(2)
-        x_turned[6] = turn_x(6, 2)
         wv_grouped[3] = regroup_weight_chunk(wv_raw[3], v_copy)
         quantise_weight_chunk(wv_grouped[2], wv_codes, wv_scales, 2)
+        for t in range(1, EARLY_TILES):
+            limit_norm(t - 1)
+            sum_of_squares(t)
+            invert_norm(t - 1)
+        x_turned[4] = turn_x(4, 2)
+        x_turned[6] = turn_x(6, 2)
         x_grouped[4] = regroup_x(x_turned[4], 2, v_copy)
         quantise_weight_chunk(wv_grouped[3], wv_codes, wv_scales, 3)
         for first in range(6, TILES, 2):
@@ -382,8 +401,14 @@ def tile_hydraencoderlayer_pa_kernel(tc, x, wk, wv, out):
             quantise_x(x_grouped[first - 2], first - 2, 2)
         quantise_x(x_grouped[TILES - 2], TILES - 2, 2)
 
+        def scalar_passes(t):
+            if is_tile(t):
+                for c in scalar_chunks(t):
+                    if (t, c) not in a_banks:
+                        key_pass(t, c, False)
+
         last_turned = []
-        for t in range(3, TILES + 1):
+        for t in range(EARLY_TILES, TILES + 1):
             if is_tile(t):
                 scalar_stage(t)
             else:
@@ -403,8 +428,7 @@ def tile_hydraencoderlayer_pa_kernel(tc, x, wk, wv, out):
                     sum_over_tokens(due[n][0], due[n][1], turn_and_add(due[n][0], due[n][1], vector_banks))
             for v in range(values_done(t - 1), values_done(t)):
                 if v == TILES - 1:
-                    for c in range(CHUNKS):
-                        value_pass(v, c)
+                    value_passes((v + 1) * CHUNKS)
                     for c in range(CHUNKS):
                         product_chunk(v, c)
                         last_turned.append(
@@ -414,8 +438,7 @@ def tile_hydraencoderlayer_pa_kernel(tc, x, wk, wv, out):
                             sum_over_tokens(LAST_GROUP, c - 1, last_turned[c - 1])
                     continue
                 if v == TILES - 2:
-                    for c in range(CHUNKS):
-                        value_pass(v, c)
+                    value_passes((v + 1) * CHUNKS)
                     for c in range(CHUNKS):
                         turn_addends(LAST_GROUP, c, scalar_banks, 0, EARLY)
                     for c in range(CHUNKS):
@@ -423,12 +446,12 @@ def tile_hydraencoderlayer_pa_kernel(tc, x, wk, wv, out):
                         add_product(v, c)
                     continue
                 for c in range(CHUNKS):
-                    value_pass(v, c)
+                    value_passes(v * CHUNKS + c + 1)
                     product_chunk(v, c)
                     add_product(v, c)
-            if is_tile(t + 1):
-                for c in scalar_chunks(t + 1):
-                    key_pass(t + 1, c, False)
+                    if v == values_done(t) - 1 and c == KPC:
+                        scalar_passes(t + 1)
+            scalar_passes(t + 1)
             if t < TILES:
                 for n in range(len(due)):
                     sum_over_tokens(due[n][0], due[n][1], turn_and_add(due[n][0], due[n][1], vector_banks))

@@ -367,10 +367,11 @@ def tile_hydraencoderlayer_pa_kernel(tc, x, wk, wv, out):
         x_grouped[1] = regroup_x(x_turned[1], 1, s_copy)
         x_grouped[2] = regroup_x(x_turned[2], 2, s_copy)
         key_copy(0, 0)
-        quantise_x(x_grouped[1], 1, 1)
-        quantise_x(x_grouped[2], 2, 2)
         for c in range(1, CHUNKS):
             wk_grouped = regroup_weight_chunk(wk_raw[c], v_copy)
+            if c == 1:
+                quantise_x(x_grouped[1], 1, 1)
+                quantise_x(x_grouped[2], 2, 2)
             for t in range(1, EARLY_TILES):
                 key_chunk(t, c - 1, False)
             quantise_weight_chunk(wk_grouped, wk_codes, wk_scales, c)

@@ -26,17 +26,18 @@ TILES = BATCHES * TOKENS // P
 KEYS = 6
 
 GROUPS = (
-    ((0, 1, 2), (3, 4, 5), (6, 7, 8)),
-    ((9, 10, 11, 12), (13, 14), (15,)),
+    ((0, 1, 2), (3, 4), (5, 6, 7)),
+    ((8, 9, 10), (11, 12), (13, 14), (15,)),
 )
 LAST_GROUP = len(GROUPS) - 1
 LAST_ADDED = 14
 EARLY = 1
 WVL = (2, 2)
 RAWB = {1: 4, 2: 2}
-VK = {5: 1, 6: 2, 7: 2, 8: 2, 9: 2, 10: 2, 11: 2, 12: 2, 13: 2, 14: 2, 15: 2}
-FIRSTV = 6
-KPC = 3
+VK = {5: 2, 6: 2, 7: 2, 8: 2, 9: 2, 10: 2, 11: 2, 12: 2, 13: 1, 14: 1, 15: 2}
+VDONE = {4: 2, 5: 4, 6: 6, 7: 7, 8: 8, 9: 9, 10: 10, 11: 11, 12: 12, 13: 13, 14: 14, 15: 15, 16: 16}
+SUMS = {11: (0,), 12: (1,), 13: (2,), 14: (3,)}
+KPC = {6: 1, 7: 1, 8: 1, 9: 1, 10: 1, 11: 1, 12: 1, 13: 1, 14: 1}
 EARLY_TILES = 4
 SUM_TIMES = ((11, 1),)
 
@@ -336,7 +337,7 @@ def tile_hydraencoderlayer_pa_kernel(tc, x, wk, wv, out):
             return range(VK.get(t, 0))
 
         def values_done(t):
-            return max(0, min(t, TILES, 2 * t - FIRSTV))
+            return VDONE.get(t, 0)
 
         def scalar_chunks(t):
             return [c for c in range(CHUNKS) if c not in vector_key_chunks(t)]
@@ -416,11 +417,7 @@ def tile_hydraencoderlayer_pa_kernel(tc, x, wk, wv, out):
                 limit_norm(t - 1)
                 invert_norm(t - 1)
             due = []
-            for g in range(LAST_GROUP):
-                first, count = SUM_TIMES[g]
-                for c in range((t - first) * count, (t - first + 1) * count):
-                    if 0 <= c < CHUNKS:
-                        due.append((g, c))
+            due = [(0, c) for c in SUMS.get(t, ())]
             if is_tile(t + 1):
                 for c in vector_key_chunks(t + 1):
                     key_chunk(t + 1, c, True)
@@ -450,7 +447,7 @@ def tile_hydraencoderlayer_pa_kernel(tc, x, wk, wv, out):
                     value_passes(v * CHUNKS + c + 1)
                     product_chunk(v, c)
                     add_product(v, c)
-                    if v == values_done(t) - 1 and c == KPC:
+                    if v == values_done(t) - 1 and c == KPC.get(t, 3):
                         scalar_passes(t + 1)
             scalar_passes(t + 1)
             if t < TILES:

from contextlib import ExitStack

import concourse.mybir as mybir
from concourse.masks import make_identity

F32 = mybir.dt.float32
BF16 = mybir.dt.bfloat16
U32 = mybir.dt.uint32
U8 = mybir.dt.uint8
FP8X4 = mybir.dt.float8_e4m3fn_x4
ALU = mybir.AluOpType
ACT = mybir.ActivationFunctionType
AXIS = mybir.AxisListType

P = 128
PACK = 4
BATCHES = 4
TOKENS = 512
FEATURES = 512
WIDTH = 2048
EPS = 1e-12
CHUNK = 512
CHUNKS = WIDTH // CHUNK
BLOCKS = CHUNK // P
TILES = BATCHES * TOKENS // P
KEYS = 6

GROUPS = (
    ((0, 1, 2), (3, 4), (5, 6, 7)),
    ((8, 9, 10), (11, 12), (13, 14), (15,)),
)
LAST_GROUP = len(GROUPS) - 1
LAST_ADDED = 14
EARLY = 1
WVL = (2, 2)
RAWB = {1: 4, 2: 2}
VK = {5: 2, 6: 2, 7: 2, 8: 2, 9: 2, 10: 2, 11: 2, 12: 2, 13: 1, 14: 1, 15: 2}
VDONE = {4: 2, 5: 4, 6: 6, 7: 7, 8: 8, 9: 9, 10: 10, 11: 11, 12: 12, 13: 13, 14: 14, 15: 15, 16: 16}
SUMS = {11: (0,), 12: (1,), 13: (2,), 14: (3,)}
KPC = {6: 1, 7: 1, 8: 1, 9: 1, 10: 1, 11: 1, 12: 1, 13: 1, 14: 1}
EARLY_TILES = 4
SUM_TIMES = ((11, 1),)

FLOPS = 2 * 2 * BATCHES * TOKENS * FEATURES * WIDTH


def tile_hydraencoderlayer_pa_kernel(tc, x, wk, wv, out):
    nc = tc.nc
    with ExitStack() as ctx:
        ctx.enter_context(tc.manual_schedule())
        keep = ctx.enter_context(tc.tile_pool(name="keep", bufs=1))
        raw_pool = ctx.enter_context(tc.tile_pool(name="raw", bufs=2 * CHUNKS))
        grouped_pool = ctx.enter_context(tc.tile_pool(name="grouped", bufs=4))
        key_pool = ctx.enter_context(tc.tile_pool(name="keys", bufs=KEYS))
        square_pool = ctx.enter_context(tc.tile_pool(name="squares", bufs=1))
        norm_pool = ctx.enter_context(tc.tile_pool(name="norms", bufs=KEYS))
        product_pool = ctx.enter_context(tc.tile_pool(name="products", bufs=2))
        addend_pool = ctx.enter_context(tc.tile_pool(name="addends", bufs=7))
        scalar_banks = ctx.enter_context(tc.psum_pool(name="scalar_banks", bufs=4))
        vector_banks = ctx.enter_context(tc.psum_pool(name="vector_banks", bufs=4))

        x_raw = keep.tile([P, TILES, FEATURES], BF16)
        x_rows = x.flatten_outer_dims().rearrange("(p t) k -> p t k", t=TILES)

        def load_x(first, count):
            tiles = slice(first, first + count)
            nc.sync.dma_start(out=x_raw[:, tiles, :], in_=x_rows[:, tiles, :])

        def load_weight_chunks(w, first, count):
            raw = raw_pool.tile([P, PACK, count * CHUNK], BF16, name="raw", tag="raw" + str(count), bufs=RAWB[count])
            nc.sync.dma_start(
                out=raw[:],
                in_=w[:, first * CHUNK : (first + count) * CHUNK].rearrange("(p t) c -> p t c", t=PACK),
            )
            return [raw[:, :, c * CHUNK : (c + 1) * CHUNK] for c in range(count)]

        def load_weights(w, counts):
            chunks = []
            for count in counts:
                chunks.extend(load_weight_chunks(w, len(chunks), count))
            return chunks

        load_x(0, 1)
        wk_raw = load_weight_chunks(wk, 0, 1)
        load_x(1, EARLY_TILES - 1)
        for c in range(1, CHUNKS):
            wk_raw.extend(load_weight_chunks(wk, c, 1))
        wv_raw = load_weights(wv, WVL)
        for first in range(4, TILES, 4):
            load_x(first, 4)

        identity = keep.tile([P, P], F32)
        make_identity(nc, identity[:])
        sums = []
        for g in range(len(GROUPS)):
            sums.append(keep.tile([P, P], F32, name="sums" + str(g)))
            nc.gpsimd.memset(sums[g][:], 0.0)
        one = keep.tile([P, 1], F32)
        nc.vector.memset(one[:], 1.0)
        nc.scalar.activation(out=one[:], in_=one[:], func=ACT.Abs_reciprocal_sqrt)
        floor = keep.tile([P, 1], F32)
        nc.vector.memset(floor[:], EPS * EPS)
        minus_floor = keep.tile([P, 1], F32)
        nc.vector.memset(minus_floor[:], -EPS * EPS)
        x_codes = keep.tile([P, TILES * P], U32, align_bytes=64)
        x_scales = keep.tile([P, TILES * P], U8, align_bytes=64)
        wk_codes = keep.tile([P, WIDTH], U32, align_bytes=64)
        wk_scales = keep.tile([P, WIDTH], U8, align_bytes=64)
        wv_codes = keep.tile([P, WIDTH], U32, align_bytes=64)
        wv_scales = keep.tile([P, WIDTH], U8, align_bytes=64)

        def turn_x(first, count):
            x_words = x_raw[:].bitcast(F32)
            flipped = vector_banks.tile([P, 2, 2, P], F32, tag="bank")
            for n in range(count):
                for u in range(2):
                    nc.tensor.transpose(
                        flipped[:, n, u, :],
                        x_words[:, first + n, u : FEATURES // 2 : 2],
                        identity[:],
                    )
            return flipped

        def regroup_x(flipped, count, copy):
            grouped = grouped_pool.tile([P, 2 * P, PACK], BF16, tag="x_grouped", bufs=3, align_bytes=64)
            grouped_words = grouped[:].bitcast(F32)
            copy(
                out=grouped_words[:, 0 : count * P, :].rearrange("p (n k) u -> p n k u", n=count),
                in_=flipped[:, 0:count].rearrange("p n u k -> p n k u"),
            )
            return grouped

        def quantise_x(grouped, first, count):
            columns = slice(first * P, (first + count) * P)
            nc.vector.quantize_mx(
                out=x_codes[:, columns].bitcast(FP8X4),
                scales=x_scales[:, columns],
                in_=grouped[:, 0 : count * P, :].rearrange("p k t -> p (k t)"),
            )

        def regroup_weight_chunk(raw, copy):
            grouped = grouped_pool.tile([P, CHUNK, PACK], BF16, tag="w_grouped", align_bytes=64)
            copy(
                out=grouped[:].rearrange("p (c i) t -> p c t i", i=4),
                in_=raw.rearrange("p t (c i) -> p c t i", i=4),
            )
            return grouped

        def quantise_weight_chunk(grouped, codes, scales, c):
            columns = slice(c * CHUNK, (c + 1) * CHUNK)
            nc.vector.quantize_mx(
                out=codes[:, columns].bitcast(FP8X4),
                scales=scales[:, columns],
                in_=grouped[:].rearrange("p c t -> p (c t)"),
            )

        keys = [None] * TILES
        norms_squared = [None] * TILES
        excess = [None] * TILES
        inverse_norms = [None] * TILES
        v_copy = nc.vector.tensor_copy
        s_copy = nc.scalar.copy
        products = [None] * TILES
        addend_of = {}
        for g in range(len(GROUPS)):
            for members in GROUPS[g]:
                for t in members:
                    addend_of[t] = members

        a_banks = {}

        def key_pass(t, c, on_vector):
            tokens = slice(t * P, (t + 1) * P)
            columns = slice(c * CHUNK, (c + 1) * CHUNK)
            if keys[t] is None:
                keys[t] = key_pool.tile([P, WIDTH], F32, name="a_sb", tag="a_sb")
            banks, copy = (vector_banks, v_copy) if on_vector else (scalar_banks, s_copy)
            a_bank = banks.tile([P, CHUNK], F32, name="a_bank", tag="bank")
            nc.tensor.matmul_mx(
                out=a_bank[:],
                lhsT=x_codes[:, tokens].bitcast(FP8X4),
                lhsT_scale=x_scales[:, tokens],
                rhs=wk_codes[:, columns].bitcast(FP8X4),
                rhs_scale=wk_scales[:, columns],
                start=True,
                stop=True,
            )
            a_banks[t, c] = (a_bank, copy)

        def key_copy(t, c):
            a_bank, copy = a_banks[t, c]
            copy(out=keys[t][:, c * CHUNK : (c + 1) * CHUNK], in_=a_bank[:])

        def key_chunk(t, c, on_vector):
            key_pass(t, c, on_vector)
            key_copy(t, c)

        def sum_of_squares(t):
            squares = square_pool.tile([P, WIDTH], BF16, tag="squares")
            first, count = norm_group(t)
            if t == first:
                norms_squared[t] = norm_pool.tile([P, 2], F32, name="norms_squared", tag="norms_squared")
            place = t - first
            nc.scalar.activation(
                out=squares[:],
                in_=keys[t][:],
                func=ACT.Square,
                accum_out=norms_squared[first][:, place : place + 1],
            )

        def norm_group(t):
            return (t, 1)

        def limit_norm(t):
            first, count = norm_group(t)
            if t != first + count - 1:
                return
            excess[first] = norm_pool.tile([P, 2], F32, name="excess", tag="excess")
            nc.scalar.activation(
                out=excess[first][:, 0:count],
                in_=norms_squared[first][:, 0:count],
                func=ACT.Relu,
                bias=minus_floor[:],
            )

        def invert_norm(t):
            first, count = norm_group(t)
            if t != first + count - 1:
                return
            inverse_norms[first] = norm_pool.tile([P, 2], F32, name="inverse_norms", tag="inverse_norms")
            nc.scalar.activation(
                out=inverse_norms[first][:, 0:count],
                in_=excess[first][:, 0:count],
                func=ACT.Abs_reciprocal_sqrt,
                bias=floor[:],
            )

        v_banks = {}
        passes = [0]

        def value_passes(upto):
            while passes[0] < min(upto, TILES * CHUNKS):
                value_pass(passes[0] // CHUNKS, passes[0] % CHUNKS)
                passes[0] += 1

        def value_pass(t, c):
            tokens = slice(t * P, (t + 1) * P)
            columns = slice(c * CHUNK, (c + 1) * CHUNK)
            v_bank = vector_banks.tile([P, CHUNK], F32, name="v_bank", tag="bank")
            nc.tensor.matmul_mx(
                out=v_bank[:],
                lhsT=x_codes[:, tokens].bitcast(FP8X4),
                lhsT_scale=x_scales[:, tokens],
                rhs=wv_codes[:, columns].bitcast(FP8X4),
                rhs_scale=wv_scales[:, columns],
                start=True,
                stop=True,
            )
            v_banks[t, c] = v_bank

        def product_chunk(t, c):
            columns = slice(c * CHUNK, (c + 1) * CHUNK)
            members = addend_of[t]
            if c == 0:
                if t == members[0]:
                    products[t] = addend_pool.tile([P, WIDTH], F32, name="addend", tag="addend")
                else:
                    products[t] = product_pool.tile([P, WIDTH], F32, name="product", tag="product")
            first, count = norm_group(t)
            nc.vector.scalar_tensor_tensor(
                out=products[t][:, columns],
                in0=keys[t][:, columns],
                scalar=inverse_norms[first][:, t - first : t - first + 1],
                in1=v_banks[t, c][:],
                op0=ALU.mult,
                op1=ALU.mult,
            )

        def add_product(t, c):
            step = 1 if t >= LAST_ADDED else CHUNKS
            members = addend_of[t]
            if t != members[0] and c % step == step - 1:
                columns = slice((c + 1 - step) * CHUNK, (c + 1) * CHUNK)
                addend = products[members[0]][:, columns]
                nc.gpsimd.tensor_tensor(
                    out=addend, in0=addend, in1=products[t][:, columns], op=ALU.add
                )

        def turn_addends(g, c, banks, first, last):
            addends = GROUPS[g]
            if first == 0:
                turned_of[g, c] = banks.tile([P, BLOCKS, P], F32, name="turned", tag="bank")
            turned = turned_of[g, c]
            for n in range(first, last):
                for j in range(BLOCKS):
                    nc.tensor.matmul(
                        out=turned[:, j, :],
                        lhsT=products[addends[n][0]][:, c * CHUNK + j * P : c * CHUNK + (j + 1) * P],
                        rhs=identity[:],
                        is_transpose=True,
                        start=n == 0 and j == 0,
                        stop=n == len(addends) - 1 and j == BLOCKS - 1,
                    )
            return turned

        turned_of = {}

        def turn_and_add(g, c, banks):
            turned = banks.tile([P, BLOCKS, P], F32, name="turned", tag="bank")
            addends = GROUPS[g]
            for j in range(BLOCKS):
                block = slice(c * CHUNK + j * P, c * CHUNK + (j + 1) * P)
                for n in range(len(addends)):
                    nc.tensor.matmul(
                        out=turned[:, j, :],
                        lhsT=products[addends[n][0]][:, block],
                        rhs=identity[:],
                        is_transpose=True,
                        start=n == 0,
                        stop=n == len(addends) - 1,
                    )
            return turned

        def sum_over_tokens(g, c, turned):
            by_batch = sums[g][:, 0 : BATCHES * CHUNKS * BLOCKS].rearrange("p (b r) -> p r b", b=BATCHES)
            nc.vector.tensor_reduce(
                out=by_batch[:, c * BLOCKS : (c + 1) * BLOCKS, :],
                in_=turned[:].rearrange("p j (b q) -> p j b q", b=BATCHES),
                axis=AXIS.X,
                op=ALU.add,
            )

        def is_tile(t):
            return 0 <= t < TILES

        def vector_key_chunks(t):
            return range(VK.get(t, 0))

        def values_done(t):
            return VDONE.get(t, 0)

        def scalar_chunks(t):
            return [c for c in range(CHUNKS) if c not in vector_key_chunks(t)]

        def scalar_stage(t):
            own = scalar_chunks(t)
            for n in range(len(own)):
                if (t, own[n]) not in a_banks:
                    key_pass(t, own[n], False)
                key_copy(t, own[n])
                if n == 0:
                    limit_norm(t - 1)
                if n == min(1, len(own) - 1):
                    invert_norm(t - 1)
            sum_of_squares(t)

        wv_grouped = [None] * CHUNKS
        x_turned = {}
        x_grouped = {}
        x_turned[0] = turn_x(0, 1)
        x_grouped[0] = regroup_x(x_turned[0], 1, s_copy)
        wk_grouped = regroup_weight_chunk(wk_raw[0], v_copy)
        quantise_x(x_grouped[0], 0, 1)
        quantise_weight_chunk(wk_grouped, wk_codes, wk_scales, 0)
        x_turned[1] = turn_x(1, 1)
        x_turned[2] = turn_x(2, 2)
        key_pass(0, 0, False)
        x_grouped[1] = regroup_x(x_turned[1], 1, s_copy)
        x_grouped[2] = regroup_x(x_turned[2], 2, s_copy)
        key_copy(0, 0)
        for c in range(1, CHUNKS):
            wk_grouped = regroup_weight_chunk(wk_raw[c], v_copy)
            if c == 1:
                quantise_x(x_grouped[1], 1, 1)
                quantise_x(x_grouped[2], 2, 2)
            for t in range(1, EARLY_TILES):
                key_chunk(t, c - 1, False)
            quantise_weight_chunk(wk_grouped, wk_codes, wk_scales, c)
            key_chunk(0, c, False)
        for t in range(1, EARLY_TILES):
            key_chunk(t, CHUNKS - 1, False)
        sum_of_squares(0)

        wv_grouped[0] = regroup_weight_chunk(wv_raw[0], v_copy)
        wv_grouped[1] = regroup_weight_chunk(wv_raw[1], v_copy)
        quantise_weight_chunk(wv_grouped[0], wv_codes, wv_scales, 0)
        wv_grouped[2] = regroup_weight_chunk(wv_raw[2], v_copy)
        quantise_weight_chunk(wv_grouped[1], wv_codes, wv_scales, 1)
        wv_grouped[3] = regroup_weight_chunk(wv_raw[3], v_copy)
        quantise_weight_chunk(wv_grouped[2], wv_codes, wv_scales, 2)
        for t in range(1, EARLY_TILES):
            limit_norm(t - 1)
            sum_of_squares(t)
            invert_norm(t - 1)
        x_turned[4] = turn_x(4, 2)
        x_turned[6] = turn_x(6, 2)
        x_grouped[4] = regroup_x(x_turned[4], 2, v_copy)
        quantise_weight_chunk(wv_grouped[3], wv_codes, wv_scales, 3)
        for first in range(6, TILES, 2):
            if first + 2 < TILES:
                x_turned[first + 2] = turn_x(first + 2, 2)
            x_grouped[first] = regroup_x(x_turned[first], 2, v_copy)
            quantise_x(x_grouped[first - 2], first - 2, 2)
        quantise_x(x_grouped[TILES - 2], TILES - 2, 2)

        def scalar_passes(t):
            if is_tile(t):
                for c in scalar_chunks(t):
                    if (t, c) not in a_banks:
                        key_pass(t, c, False)

        last_turned = []
        for t in range(EARLY_TILES, TILES + 1):
            if is_tile(t):
                scalar_stage(t)
            else:
                limit_norm(t - 1)
                invert_norm(t - 1)
            due = []
            due = [(0, c) for c in SUMS.get(t, ())]
            if is_tile(t + 1):
                for c in vector_key_chunks(t + 1):
                    key_chunk(t + 1, c, True)
            if t == TILES:
                for n in range(len(due)):
                    sum_over_tokens(due[n][0], due[n][1], turn_and_add(due[n][0], due[n][1], vector_banks))
            for v in range(values_done(t - 1), values_done(t)):
                if v == TILES - 1:
                    value_passes((v + 1) * CHUNKS)
                    for c in range(CHUNKS):
                        product_chunk(v, c)
                        last_turned.append(
                            turn_addends(LAST_GROUP, c, scalar_banks, EARLY, len(GROUPS[LAST_GROUP]))
                        )
                        if c > 0:
                            sum_over_tokens(LAST_GROUP, c - 1, last_turned[c - 1])
                    continue
                if v == TILES - 2:
                    value_passes((v + 1) * CHUNKS)
                    for c in range(CHUNKS):
                        turn_addends(LAST_GROUP, c, scalar_banks, 0, EARLY)
                    for c in range(CHUNKS):
                        product_chunk(v, c)
                        add_product(v, c)
                    continue
                for c in range(CHUNKS):
                    value_passes(v * CHUNKS + c + 1)
                    product_chunk(v, c)
                    add_product(v, c)
                    if v == values_done(t) - 1 and c == KPC.get(t, 3):
                        scalar_passes(t + 1)
            scalar_passes(t + 1)
            if t < TILES:
                for n in range(len(due)):
                    sum_over_tokens(due[n][0], due[n][1], turn_and_add(due[n][0], due[n][1], vector_banks))
        sum_over_tokens(LAST_GROUP, CHUNKS - 1, last_turned[CHUNKS - 1])

        rows = BATCHES * CHUNKS * BLOCKS
        turned_sums = scalar_banks.tile([P, P], F32, tag="bank")
        for g in range(len(GROUPS)):
            nc.tensor.matmul(
                out=turned_sums[:],
                lhsT=sums[g][:],
                rhs=identity[:],
                is_transpose=True,
                start=g == 0,
                stop=g == len(GROUPS) - 1,
            )
        result = keep.tile([P, P], F32)
        nc.vector.tensor_copy(out=result[:], in_=turned_sums[:])
        nc.sync.dma_start(out=out.rearrange("b o (r p) -> (b o r) p", p=P), in_=result[0:rows, :])
